import numpy as np
import ml_dtypes


def mxq(x, axis, fmt="e4m3"):
    dtype, down = {"e4m3": (ml_dtypes.float8_e4m3fn, 7), "e5m2": (ml_dtypes.float8_e5m2, 14)}[fmt]
    v = np.moveaxis(np.asarray(x, np.float32).astype(ml_dtypes.bfloat16).astype(np.float64), axis, -1)
    blocks = v.reshape(v.shape[:-1] + (-1, 32))
    amax = np.abs(blocks).max(-1, keepdims=True)
    byte = np.maximum(np.where(amax > 0, np.frexp(amax)[1] - 1 + 127, 0) - down, 1)
    scale = np.exp2(byte - 127.0)
    codes = (blocks / scale).astype(np.float32).astype(dtype).astype(np.float64)
    return np.moveaxis((codes * scale).reshape(v.shape), -1, axis)


WIDE = False


def mx_kscale(k):
    if not WIDE:
        return np.ones(k)
    levels = np.array([10, -10, 5, -5, 0])
    if k % 512:
        return np.exp2(np.random.permutation(np.resize(levels, k // 32))).repeat(32)
    a = np.empty((k // 512, 16))
    for p in range(k // 512):
        a[p, :8] = np.random.permutation(np.resize(levels, 8))
        for g in range(8):
            far = levels[np.abs(levels - a[p, g]) >= 10]
            a[p, g + 8] = far[np.random.randint(len(far))]
    return np.exp2(a.ravel()).repeat(32)


BF16 = ml_dtypes.bfloat16


def bf(x):
    return np.asarray(x, np.float32).astype(BF16)


def f64(x):
    return np.asarray(x).astype(np.float64)


E2M1 = np.array([0.0, 0.5, 1.0, 1.5, 2.0, 3.0, 4.0, 6.0, -0.0, -0.5, -1.0, -1.5, -2.0, -3.0, -4.0, -6.0])


def pack_weight(w, fmt):
    k, n = w.shape
    w = f64(bf(w)).reshape(k // 32, 32, n)
    amax = np.abs(w).max(1)
    if fmt == "e4m3":
        byte = np.frexp(amax)[1] - 1 + 127 - 7
    else:
        mant, ex = np.frexp(amax / 6.0)
        byte = np.where(mant > 0.5, ex, ex - 1) + 127
    byte = np.clip(np.where(amax > 0, byte, 1), 1, 254)
    scaled = (w * np.exp2(127.0 - byte)[:, None, :]).reshape(k, n).astype(np.float32)
    by_word = np.ascontiguousarray(scaled.reshape(k // 512, 128, 4, n).transpose(0, 1, 3, 2))
    if fmt == "e4m3":
        words = by_word.astype(ml_dtypes.float8_e4m3fn).view(np.uint8)
    else:
        c = by_word.astype(ml_dtypes.float4_e2m1fn).view(np.uint8) & 0xF
        words = c[..., 0::2] | (c[..., 1::2] << 4)
    return np.ascontiguousarray(words), np.ascontiguousarray(byte.astype(np.uint8).reshape(k // 512, 16, n))


def unpack_weight(words, scales, fmt):
    g, p, n, _ = words.shape
    if fmt == "e4m3":
        vals = np.ascontiguousarray(words).view(ml_dtypes.float8_e4m3fn).astype(np.float64)
    else:
        nib = np.empty((g, p, n, 4), np.uint8)
        nib[..., 0::2] = words & 0xF
        nib[..., 1::2] = words >> 4
        vals = E2M1[nib]
    vals = vals * np.repeat(np.exp2(scales.astype(np.float64) - 127.0), 8, axis=1)[..., None]
    return vals.transpose(0, 1, 3, 2).reshape(g * 512, n)
def pack4(w):
    words, scales = pack_weight(w, "e2m1")
    return words.reshape(words.shape[0], 128, -1), scales


def unpack4(words, scales):
    return unpack_weight(words.reshape(words.shape[0], 128, -1, 2), scales, "e2m1")


B, K, G, D, FF, F, P, H = 16, 64, 128, 1024, 2048, 2048, 7, 8
NC = K * G
EPS = 1e-5


def layernorm(x, g, b):
    m = x.mean(-1, keepdims=True)
    v = ((x - m) ** 2).mean(-1, keepdims=True)
    return (x - m) / np.sqrt(v + EPS) * g + b


def draw0():
    n = np.random.standard_normal
    s, t = mx_kscale(FF), mx_kscale(D)
    ff_hid = bf(np.maximum(n((B, K, FF)), 0.0) * s)
    tgt = bf(n((B, K, D)))
    words, scales = pack4(n((FF, D)) / np.sqrt(FF) / s[:, None])
    return {
        "ff_hid": ff_hid,
        "tgt": tgt,
        "w2_words": words,
        "w2_scales": scales,
        "b2": bf(0.1 * n(D)),
        "g3": bf((1.0 + 0.1 * n(D)) * t),
        "be3": bf(0.1 * n(D) * t),
        "dup_pool": bf(n((K, D, G)) / np.sqrt(D) / t[None, :, None]),
        "dup_bias": bf(0.2 * n(NC)),
    }


def core(ff_hid, tgt, w2_words, w2_scales, b2, g3, be3, dup_pool, dup_bias):
    ff = (mxq(f64(ff_hid), 2, "e4m3") @ unpack4(w2_words, w2_scales)) + f64(b2)
    h = layernorm(f64(tgt) + ff, f64(g3), f64(be3))
    out_extrap = (mxq(h, 2, "e4m3").transpose(1, 0, 2) @ mxq(f64(dup_pool), 1, "e4m3")).transpose(1, 0, 2)
    return out_extrap.reshape(B, -1)[:, :NC] + f64(dup_bias)


def e4m3fn_bytes(y):
    return np.clip(np.asarray(y, np.float64), -448.0, 448.0).astype(np.float32).astype(ml_dtypes.float8_e4m3fn).view(np.uint8)


def e4m3fn_values(b):
    return np.asarray(b, np.uint8).view(ml_dtypes.float8_e4m3fn).astype(np.float64)


def setup_inputs():
    d = draw0()
    x0 = np.asarray(d['dup_pool']).astype(np.float64)
    s = (np.max(np.abs(x0), axis=(0, 2), keepdims=True) / 448.0).astype(np.float32)
    out = {}
    for k, v in d.items():
        if k == 'dup_pool':
            out['dup_pool_bytes'] = e4m3fn_bytes(x0 / s.astype(np.float64))
            out['dup_pool_scale'] = s
        else:
            out[k] = v
    return out


def reference(ff_hid, tgt, w2_words, w2_scales, b2, g3, be3, dup_pool_bytes, dup_pool_scale, dup_bias):
    return core(ff_hid, tgt, w2_words, w2_scales, b2, g3, be3, e4m3fn_values(dup_pool_bytes) * dup_pool_scale.astype(np.float64), dup_bias)

@@ -1,0 +1,363 @@
+from contextlib import ExitStack
+
+import concourse.mybir as mybir
+from concourse.masks import make_identity
+
+B, K, G, D, FF = 16, 64, 128, 1024, 2048
+FLOPS = 2 * B * K * FF * D + 2 * B * K * D * G
+
+F32 = mybir.dt.float32
+BF16 = mybir.dt.bfloat16
+U32 = mybir.dt.uint32
+I32 = mybir.dt.int32
+U8 = mybir.dt.uint8
+FP8 = mybir.dt.float8_e4m3fn
+FP8X4 = mybir.dt.float8_e4m3fn_x4
+FP4X4 = mybir.dt.float4_e2m1fn_x4
+ACT = mybir.ActivationFunctionType
+ALU = mybir.AluOpType
+
+P = 128
+NT = 8
+KL = 8
+EPS = 1e-5
+
+
+def tile_mldecoder_pb_w4_kernel(
+    tc, ff_hid, tgt, w2_words, w2_scales, b2, g3, be3, dup_pool_bytes, dup_pool_scale, dup_bias, out
+):
+    nc = tc.nc
+    ff_g = ff_hid.rearrange("b k f -> (b k) f").rearrange("(m kt) f -> kt m f", kt=NT)
+    tgt_g = tgt.rearrange("b k f -> (b k) f").rearrange("(m kt) f -> kt m f", kt=NT)
+    dup_g = dup_pool_bytes.rearrange("(kl kt) (g p t) n -> kt g t p kl n", kt=NT, g=2, t=4)
+    out_g = out.rearrange("b (kl kt g) -> kt (b kl) g", kt=NT, kl=KL)
+
+    with ExitStack() as ctx:
+        keep = ctx.enter_context(tc.tile_pool(name="keep", bufs=1))
+        sb = ctx.enter_context(tc.tile_pool(name="sb", bufs=2))
+        psum = ctx.enter_context(tc.psum_pool(name="psum", bufs=2))
+        ctx.enter_context(tc.manual_schedule())
+
+        raw, xf, tg, wd, gd, dc, ds = {}, {}, {}, {}, {}, {}, {}
+        xt, xg, fc, fs, acc, tb, st = {}, {}, {}, {}, {}, {}, {}
+        us, zs, ht, hp, hg, hc, hs = {}, {}, {}, {}, {}, {}, {}
+        so, res, oT = {}, {}, {}
+
+        def load_dup(T, g):
+            for t in range(4):
+                r = sb.tile([P, KL * G], U8, name="raw", tag="raw", bufs=24, align_bytes=64)
+                nc.sync.dma_start(out=r[:].rearrange("p (kl n) -> p kl n", kl=KL), in_=dup_g[T][g][t])
+                raw[T, g, t] = r
+
+        def load_ff(T):
+            x = sb.tile([P, FF], BF16, name="xf", tag="xf", bufs=3, align_bytes=64)
+            nc.sync.dma_start(out=x[:], in_=ff_g[T])
+            xf[T] = x
+
+        def load_tgt(T):
+            x = sb.tile([P, D], BF16, name="tg", tag="tg", bufs=3, align_bytes=64)
+            nc.sync.dma_start(out=x[:], in_=tgt_g[T])
+            tg[T] = x
+
+        dsc = keep.tile([P, 2, 4], F32, name="dsc")
+        nc.sync.dma_start(out=dsc[:], in_=dup_pool_scale.rearrange("o (g p t) u -> p (o g) (t u)", g=2, t=4))
+        b2r = keep.tile([P, D], BF16, name="b2r", align_bytes=64)
+        nc.vector.memset(b2r[:], 0.0)
+        nc.gpsimd.dma_start(out=b2r[0:1, :], in_=b2.unsqueeze(0))
+        gb = keep.tile([P, 2, 4], BF16, name="gb")
+        bb = keep.tile([P, 2, 4], BF16, name="bb")
+        nc.gpsimd.dma_start(out=gb[:], in_=g3.rearrange("(g p t) -> p g t", g=2, t=4))
+        nc.gpsimd.dma_start(out=bb[:], in_=be3.rearrange("(g p t) -> p g t", g=2, t=4))
+        ident = keep.tile([P, P], F32, name="ident")
+        make_identity(nc, ident[:])
+        brow = keep.tile([P, P], BF16, name="brow", align_bytes=64)
+        nc.gpsimd.memset(brow[:], 0.0)
+        nc.gpsimd.dma_start(out=brow[0:K, :], in_=dup_bias.rearrange("(k g) -> k g", g=G))
+        ones = keep.tile([P, P], BF16, name="ones")
+        nc.vector.memset(ones[:], 1.0)
+        warm = keep.tile([P, 1], F32, name="warm")
+        nc.scalar.activation(out=warm[:], in_=ones[:, 0:1], func=ACT.Sqrt)
+        w2w = keep.tile([P, 4, 2 * D], U8, name="w2w", align_bytes=64)
+        w2s = keep.tile([P, 4, D], U8, name="w2s", align_bytes=64)
+        nc.vector.memset(w2s[:].rearrange("p g n -> p (g n)").bitcast(I32), 0)
+        gf = keep.tile([P, 2, 4], F32, name="gf")
+        bf = keep.tile([P, 2, 4], F32, name="bf")
+        biasT = keep.tile([P, K], F32, name="biasT")
+        b2b = keep.tile([P, D], F32, name="b2b")
+        browf = keep.tile([P, P], F32, name="browf")
+
+        def load_w2():
+            nc.sync.dma_start(out=w2w[:], in_=w2_words.rearrange("g p n -> p g n"))
+
+        def load_w2s():
+            for Q in range(4):
+                nc.sync.dma_start(
+                    out=w2s[32 * Q : 32 * Q + 4, :, :].bitcast(I32),
+                    in_=w2_scales[:, 4 * Q : 4 * Q + 4, :].rearrange("g q n -> q g n").bitcast(I32),
+                )
+
+        def widen(eng, T, g, t):
+            if (T, g) not in wd:
+                wd[T, g] = sb.tile([P, 4, KL * G], BF16, name="wd", tag="wd", bufs=3, align_bytes=64)
+            src = raw[T, g, t][:].bitcast(FP8)
+            dst = wd[T, g][:, t, :]
+            if eng == "S":
+                nc.scalar.activation(out=dst, in_=src, func=ACT.Copy, scale=dsc[:, g, t : t + 1])
+            else:
+                nc.vector.tensor_scalar(out=dst, in0=src, scalar1=dsc[:, g, t : t + 1], scalar2=None, op0=ALU.mult)
+
+        def inter_dup(T, g):
+            y = sb.tile([P, KL * G * 4], BF16, name="gd", tag="gd", bufs=3, align_bytes=64)
+            nc.vector.tensor_copy(
+                out=y[:].rearrange("p (c i t) -> p c t i", i=4, t=4),
+                in_=wd[T, g][:].rearrange("p t (c i) -> p c t i", i=4),
+            )
+            gd[T, g] = y
+
+        def quant_dup(T, g):
+            c = sb.tile([P, KL * G], U32, name="dc", tag="dc", bufs=8, align_bytes=64)
+            s = sb.tile([P, KL * G], U8, name="ds", tag="ds", bufs=8, align_bytes=64)
+            nc.vector.quantize_mx(out=c[:].bitcast(FP8X4), scales=s[:], in_=gd[T, g][:])
+            dc[T, g], ds[T, g] = c, s
+
+        def xpose_ff(T):
+            words = xf[T][:].bitcast(F32)
+            for j in range(2):
+                x = psum.tile([P, 512], F32, name="xt", tag="xt", bufs=2)
+                for gg in range(2):
+                    for u in range(2):
+                        lo = 256 * (2 * j + gg) + u
+                        nc.tensor.transpose(
+                            x[:, 256 * gg + 128 * u : 256 * gg + 128 * u + 128], words[:, lo : lo + 255 : 2], ident[:]
+                        )
+                xt[T, j] = x
+
+        def evac_ff(T):
+            y = sb.tile([P, 4 * P * 4], BF16, name="xg", tag="xg", bufs=2, align_bytes=64)
+            for j in range(2):
+                nc.scalar.copy(
+                    out=y[:, 1024 * j : 1024 * (j + 1)].bitcast(F32).rearrange("p (g r u) -> p g r u", g=2, u=2),
+                    in_=xt[T, j][:].rearrange("p (g u r) -> p g r u", g=2, u=2),
+                )
+            xg[T] = y
+
+        def quant_ff(T):
+            c = sb.tile([P, 4 * P], U32, name="fc", tag="fc", bufs=2, align_bytes=64)
+            s = sb.tile([P, 4 * P], U8, name="fs", tag="fs", bufs=2, align_bytes=64)
+            nc.vector.quantize_mx(out=c[:].bitcast(FP8X4), scales=s[:], in_=xg[T][:])
+            fc[T], fs[T] = c, s
+
+        def stage1(T):
+            for h in range(2):
+                a = psum.tile([P, 512], F32, name="acc", tag="acc", bufs=2)
+                for g in range(4):
+                    nc.tensor.matmul_mx(
+                        out=a[:],
+                        lhsT=fc[T][:, P * g : P * (g + 1)].bitcast(FP8X4),
+                        lhsT_scale=fs[T][:, P * g : P * (g + 1)],
+                        rhs=w2w[:, g, 1024 * h : 1024 * (h + 1)].bitcast(FP4X4),
+                        rhs_scale=w2s[:, g, 512 * h : 512 * (h + 1)],
+                        start=(g == 0),
+                        stop=(g == 3),
+                    )
+                acc[T, h] = a
+
+        def tgtb(T):
+            y = sb.tile([P, D], F32, name="tb", tag="tb", bufs=2, align_bytes=64)
+            nc.vector.tensor_tensor(out=y[:], in0=tg[T][:], in1=b2b[:], op=ALU.add)
+            tb[T] = y
+
+        def resid(T):
+            y = sb.tile([P, D], F32, name="us", tag="us", bufs=2, align_bytes=64)
+            a = []
+            for h in range(2):
+                s = sb.tile([P, 1], F32, name="sum", tag="sum" + str(h), bufs=2)
+                nc.vector.scalar_tensor_tensor(
+                    out=y[:, 512 * h : 512 * (h + 1)], in0=acc[T, h][:], scalar=0.0,
+                    in1=tb[T][:, 512 * h : 512 * (h + 1)], op0=ALU.add, op1=ALU.add, accum_out=s[:],
+                )
+                a.append(s)
+            m = sb.tile([P, 1], F32, name="nm", tag="nm", bufs=2)
+            nc.vector.tensor_scalar(
+                out=m[:], in0=a[0][:], scalar1=a[1][:], scalar2=-1.0 / D, op0=ALU.add, op1=ALU.mult
+            )
+            us[T], st[T] = y, m
+
+        def square(T):
+            junk = sb.tile([P, D], F32, name="junk", tag="junk", bufs=1)
+            ss = sb.tile([P, 1], F32, name="ss", tag="ss", bufs=2)
+            nc.scalar.activation(out=junk[:], in_=us[T][:], func=ACT.Square, bias=st[T][:], accum_out=ss[:])
+            sd = sb.tile([P, 1], F32, name="sd", tag="sd", bufs=2)
+            nc.scalar.activation(out=sd[:], in_=ss[:], func=ACT.Sqrt, scale=1.0 / D, bias=EPS)
+            st[T] = (st[T], sd)
+
+        def norm(T):
+            m, sd = st[T]
+            r = sb.tile([P, 1], F32, name="rs", tag="rs", bufs=2)
+            nc.vector.reciprocal(out=r[:], in_=sd[:])
+            y = sb.tile([P, D], F32, name="zs", tag="zs", bufs=2, align_bytes=64)
+            nc.vector.tensor_scalar(
+                out=y[:], in0=us[T][:], scalar1=m[:], scalar2=r[:], op0=ALU.add, op1=ALU.mult
+            )
+            zs[T] = y
+
+        def xpose_z(T):
+            for g in range(2):
+                x = psum.tile([P, 512], F32, name="ht", tag="ht", bufs=2)
+                for t in range(4):
+                    lo = 512 * g + t
+                    nc.tensor.transpose(x[:, P * t : P * (t + 1)], zs[T][:, lo : lo + 509 : 4], ident[:])
+                ht[T, g] = x
+
+        def evac_h(T):
+            y = sb.tile([P, 2, 4, P], BF16, name="hp", tag="hp", bufs=2, align_bytes=64)
+            for g in range(2):
+                for t in range(4):
+                    nc.scalar.activation(
+                        out=y[:, g, t, :], in_=ht[T, g][:, P * t : P * (t + 1)], func=ACT.Identity,
+                        scale=gf[:, g, t : t + 1], bias=bf[:, g, t : t + 1],
+                    )
+            hp[T] = y
+
+        def inter_h(T):
+            y = sb.tile([P, 2 * P * 4], BF16, name="hg", tag="hg", bufs=2, align_bytes=64)
+            for g in range(2):
+                nc.vector.tensor_copy(
+                    out=y[:, 512 * g : 512 * (g + 1)].rearrange("p (kl b t) -> p kl b t", kl=KL, t=4),
+                    in_=hp[T][:, g, :, :].rearrange("p t (b kl) -> p kl b t", kl=KL),
+                )
+            hg[T] = y
+
+        def quant_h(T):
+            c = sb.tile([P, 2 * P], U32, name="hc", tag="hc", bufs=4, align_bytes=64)
+            s = sb.tile([P, 2 * P], U8, name="hs", tag="hs", bufs=4, align_bytes=64)
+            nc.vector.quantize_mx(out=c[:].bitcast(FP8X4), scales=s[:], in_=hg[T][:])
+            hc[T], hs[T] = c, s
+
+        def stage2(T):
+            for h in range(2):
+                a = psum.tile([P, 512], F32, name="so", tag="so", bufs=2)
+                for j in range(4):
+                    kl = 4 * h + j
+                    for g in range(2):
+                        nc.tensor.matmul_mx(
+                            out=a[:, P * j : P * (j + 1)],
+                            lhsT=dc[T, g][:, P * kl : P * (kl + 1)].bitcast(FP8X4),
+                            lhsT_scale=ds[T, g][:, P * kl : P * (kl + 1)],
+                            rhs=hc[T][:, P * g : P * (g + 1)].bitcast(FP8X4),
+                            rhs_scale=hs[T][:, P * g : P * (g + 1)],
+                            start=(g == 0),
+                            stop=(g == 1),
+                        )
+                so[T, h] = a
+
+        def evac_out(T):
+            y = sb.tile([P, P], F32, name="res", tag="res", bufs=2, align_bytes=64)
+            yv = y[:].rearrange("p (b kl) -> p kl b", kl=KL)
+            bv = biasT[:].rearrange("p (kl kt) -> p kl kt", kt=NT)
+            for h in range(2):
+                v = so[T, h][:, 64 * h : 64 * h + 448].rearrange("p (a c) -> p a c", c=16)[:, 0:28:9, :]
+                nc.vector.tensor_tensor(
+                    out=yv[:, 4 * h : 4 * h + 4, :], in0=v,
+                    in1=bv[:, 4 * h : 4 * h + 4, T : T + 1].to_broadcast([P, 4, B]), op=ALU.add,
+                )
+            res[T] = y
+
+        def xpose_out(T):
+            x = psum.tile([P, 512], F32, name="so", tag="so", bufs=2)
+            nc.tensor.transpose(x[:, 0:P], res[T][:], ident[:])
+            oT[T] = x
+
+        def copy_out(T):
+            y = sb.tile([P, G], F32, name="ot", tag="ot", bufs=2, align_bytes=64)
+            nc.scalar.copy(out=y[:], in_=oT[T][:, 0:P])
+            nc.scalar.dma_start(out=out_g[T], in_=y[:])
+
+        NU = 2 * NT
+        VW = {(2 * i + 1, 3) for i in range(0, NT)}
+        S_OF = [2 + (11 * T + 3) // 7 for T in range(NT)]
+        O_AT = {max(2 * T + 2, S_OF[T] + 2): T for T in range(NT)}
+        LN_AT = {S_OF[T]: T for T in range(NT)}
+
+        def load_unit(n):
+            load_dup(n // 2, n % 2)
+
+        def wid(n, ts):
+            if n < NU:
+                for t in ts:
+                    if (n, t) not in VW:
+                        widen("S", n // 2, n % 2, t)
+
+        def widv(n):
+            if n < NU:
+                for t in range(4):
+                    if (n, t) in VW:
+                        widen("V", n // 2, n % 2, t)
+
+        def out_at(n, f):
+            if n in O_AT:
+                f(O_AT[n])
+
+        def at(n, f):
+            if n in LN_AT:
+                f(LN_AT[n])
+
+        load_unit(0)
+        load_ff(0)
+        load_unit(1)
+        load_w2()
+        load_w2s()
+        load_tgt(0)
+        load_unit(2)
+        widen("S", 0, 0, 0)
+        widen("S", 0, 0, 2)
+        widen("V", 0, 0, 1)
+        widen("V", 0, 0, 3)
+        bp = psum.tile([P, 512], F32, name="so", tag="so", bufs=2)
+        nc.vector.tensor_copy(out=browf[:], in_=brow[:])
+        nc.tensor.transpose(bp[:, 0:P], browf[:], ident[:])
+        nc.vector.tensor_copy(out=gf[:], in_=gb[:])
+        nc.vector.tensor_copy(out=bf[:], in_=bb[:])
+        b2p = []
+        for h in range(2):
+            x = psum.tile([P, 512], F32, name="acc", tag="acc", bufs=2)
+            nc.tensor.matmul(x[:], lhsT=ones[:], rhs=b2r[:, 512 * h : 512 * (h + 1)], start=True, stop=True)
+            b2p.append(x)
+        for h in range(2):
+            nc.vector.tensor_copy(out=b2b[:, 512 * h : 512 * (h + 1)], in_=b2p[h][:])
+        nc.vector.tensor_copy(out=biasT[:], in_=bp[:, 0:K])
+
+        for n in range(NU):
+            if n + 3 < NU:
+                load_unit(n + 3)
+            if n + 4 in LN_AT and LN_AT[n + 4] > 0:
+                load_ff(LN_AT[n + 4])
+                load_tgt(LN_AT[n + 4])
+            at(n + 2, xpose_ff)
+            at(n - 1, norm)
+            at(n - 1, xpose_z)
+            at(n, resid)
+            wid(n + 1, (0, 1))
+            at(n + 1, quant_ff)
+            at(n + 1, stage1)
+            at(n + 2, evac_ff)
+            at(n, square)
+            at(n - 1, evac_h)
+            inter_dup(n // 2, n % 2)
+            at(n - 2, inter_h)
+            out_at(n - 1, evac_out)
+            out_at(n - 1, xpose_out)
+            at(n + 1, tgtb)
+            wid(n + 1, (2,))
+            out_at(n - 1, copy_out)
+            if n > 0:
+                quant_dup((n - 1) // 2, (n - 1) % 2)
+            at(n - 2, quant_h)
+            wid(n + 1, (3,))
+            widv(n + 1)
+            out_at(n, stage2)
+        quant_dup(NT - 1, 1)
+        stage2(NT - 1)
+        evac_out(NT - 1)
+        xpose_out(NT - 1)
+        copy_out(NT - 1)

@@ -20,7 +20,12 @@ ALU = mybir.AluOpType
 P = 128
 NT = 8
 KL = 8
+NU = 2 * NT
 EPS = 1e-5
+S_OF = [2 + (11 * T + 3) // 7 for T in range(NT)]
+LN_AT = {S_OF[T]: T for T in range(NT)}
+O_AT = {max(2 * T + 2, S_OF[T] + 2): T for T in range(NT)}
+V_TGT = (0, 1)
 
 
 def tile_mldecoder_pb_w4_kernel(
@@ -29,7 +34,7 @@ def tile_mldecoder_pb_w4_kernel(
     nc = tc.nc
     ff_g = ff_hid.rearrange("b k f -> (b k) f").rearrange("(m kt) f -> kt m f", kt=NT)
     tgt_g = tgt.rearrange("b k f -> (b k) f").rearrange("(m kt) f -> kt m f", kt=NT)
-    dup_g = dup_pool_bytes.rearrange("(kl kt) (g p t) n -> kt g t p kl n", kt=NT, g=2, t=4)
+    dup_g = dup_pool_bytes.rearrange("(kl kt) (g p t) n -> kt g p kl (t n)", kt=NT, g=2, t=4)
     out_g = out.rearrange("b (kl kt g) -> kt (b kl) g", kt=NT, kl=KL)
 
     with ExitStack() as ctx:
@@ -39,15 +44,19 @@ def tile_mldecoder_pb_w4_kernel(
         ctx.enter_context(tc.manual_schedule())
 
         raw, xf, tg, wd, gd, dc, ds = {}, {}, {}, {}, {}, {}, {}
-        xt, xg, fc, fs, acc, tb, st = {}, {}, {}, {}, {}, {}, {}
-        us, zs, ht, hp, hg, hc, hs = {}, {}, {}, {}, {}, {}, {}
+        xt, xg, fc, fs, acc, tb, tp = {}, {}, {}, {}, {}, {}, {}
+        us, sm, nm, sd, rs, zs, ht, hp, hg, hc, hs = {}, {}, {}, {}, {}, {}, {}, {}, {}, {}, {}
         so, res, oT = {}, {}, {}
 
-        def load_dup(T, g):
-            for t in range(4):
-                r = sb.tile([P, KL * G], U8, name="raw", tag="raw", bufs=24, align_bytes=64)
-                nc.sync.dma_start(out=r[:].rearrange("p (kl n) -> p kl n", kl=KL), in_=dup_g[T][g][t])
-                raw[T, g, t] = r
+        def load_unit(n, parts=1):
+            w = KL // parts
+            for q in range(parts):
+                r = sb.tile([P, w * 4 * G], U8, name="raw", tag="raw" + str(parts), bufs=6 if parts == 1 else parts, align_bytes=64)
+                nc.sync.dma_start(
+                    out=r[:].rearrange("p (kl x) -> p kl x", kl=w), in_=dup_g[n // 2][n % 2][:, w * q : w * (q + 1), :]
+                )
+                for j in range(w):
+                    raw[n, w * q + j] = (r, j)
 
         def load_ff(T):
             x = sb.tile([P, FF], BF16, name="xf", tag="xf", bufs=3, align_bytes=64)
@@ -61,6 +70,7 @@ def tile_mldecoder_pb_w4_kernel(
 
         dsc = keep.tile([P, 2, 4], F32, name="dsc")
         nc.sync.dma_start(out=dsc[:], in_=dup_pool_scale.rearrange("o (g p t) u -> p (o g) (t u)", g=2, t=4))
+        load_unit(0, 4)
         b2r = keep.tile([P, D], BF16, name="b2r", align_bytes=64)
         nc.vector.memset(b2r[:], 0.0)
         nc.gpsimd.dma_start(out=b2r[0:1, :], in_=b2.unsqueeze(0))
@@ -85,6 +95,7 @@ def tile_mldecoder_pb_w4_kernel(
         biasT = keep.tile([P, K], F32, name="biasT")
         b2b = keep.tile([P, D], F32, name="b2b")
         browf = keep.tile([P, P], F32, name="browf")
+        identb = keep.tile([P, P], BF16, name="identb")
 
         def load_w2():
             nc.sync.dma_start(out=w2w[:], in_=w2_words.rearrange("g p n -> p g n"))
@@ -96,29 +107,46 @@ def tile_mldecoder_pb_w4_kernel(
                     in_=w2_scales[:, 4 * Q : 4 * Q + 4, :].rearrange("g q n -> q g n").bitcast(I32),
                 )
 
-        def widen(eng, T, g, t):
-            if (T, g) not in wd:
-                wd[T, g] = sb.tile([P, 4, KL * G], BF16, name="wd", tag="wd", bufs=3, align_bytes=64)
-            src = raw[T, g, t][:].bitcast(FP8)
-            dst = wd[T, g][:, t, :]
-            if eng == "S":
-                nc.scalar.activation(out=dst, in_=src, func=ACT.Copy, scale=dsc[:, g, t : t + 1])
-            else:
-                nc.vector.tensor_scalar(out=dst, in0=src, scalar1=dsc[:, g, t : t + 1], scalar2=None, op0=ALU.mult)
+        def vk(n):
+            return 4 if n < 2 else 1 + n % 2
 
-        def inter_dup(T, g):
+        def widen(eng, n, t, kls):
+            if n not in wd:
+                wd[n] = sb.tile([P, 4, KL * G], BF16, name="wd", tag="wd", bufs=3, align_bytes=64)
+            for kl in kls:
+                r, j = raw[n, kl]
+                lo = (4 * j + t) * G
+                src = r[:, lo : lo + G].bitcast(FP8)
+                dst = wd[n][:, t, kl * G : (kl + 1) * G]
+                scale = dsc[:, n % 2, t : t + 1]
+                if eng == "S":
+                    nc.scalar.activation(out=dst, in_=src, func=ACT.Copy, scale=scale)
+                else:
+                    nc.vector.tensor_scalar(out=dst, in0=src, scalar1=scale, scalar2=None, op0=ALU.mult)
+
+        def wid(n, ts):
+            if n < NU:
+                for t in ts:
+                    widen("S", n, t, range(KL - vk(n)))
+
+        def widv(n):
+            if n < NU:
+                for t in range(4):
+                    widen("V", n, t, range(KL - vk(n), KL))
+
+        def inter_dup(n):
             y = sb.tile([P, KL * G * 4], BF16, name="gd", tag="gd", bufs=3, align_bytes=64)
             nc.vector.tensor_copy(
                 out=y[:].rearrange("p (c i t) -> p c t i", i=4, t=4),
-                in_=wd[T, g][:].rearrange("p t (c i) -> p c t i", i=4),
+                in_=wd[n][:].rearrange("p t (c i) -> p c t i", i=4),
             )
-            gd[T, g] = y
+            gd[n] = y
 
-        def quant_dup(T, g):
+        def quant_dup(n):
             c = sb.tile([P, KL * G], U32, name="dc", tag="dc", bufs=8, align_bytes=64)
             s = sb.tile([P, KL * G], U8, name="ds", tag="ds", bufs=8, align_bytes=64)
-            nc.vector.quantize_mx(out=c[:].bitcast(FP8X4), scales=s[:], in_=gd[T, g][:])
-            dc[T, g], ds[T, g] = c, s
+            nc.vector.quantize_mx(out=c[:].bitcast(FP8X4), scales=s[:], in_=gd[n][:])
+            dc[n], ds[n] = c, s
 
         def xpose_ff(T):
             words = xf[T][:].bitcast(F32)
@@ -162,42 +190,59 @@ def tile_mldecoder_pb_w4_kernel(
                     )
                 acc[T, h] = a
 
+        def tgt_mm(T):
+            if T not in V_TGT:
+                for h in range(2):
+                    x = psum.tile([P, 512], F32, name="xt", tag="xt", bufs=2)
+                    cols = slice(512 * h, 512 * (h + 1))
+                    nc.tensor.matmul(x[:], lhsT=identb[:], rhs=tg[T][:, cols], start=True, stop=False)
+                    nc.tensor.matmul(x[:], lhsT=ones[:], rhs=b2r[:, cols], start=False, stop=True)
+                    tp[T, h] = x
+
         def tgtb(T):
             y = sb.tile([P, D], F32, name="tb", tag="tb", bufs=2, align_bytes=64)
-            nc.vector.tensor_tensor(out=y[:], in0=tg[T][:], in1=b2b[:], op=ALU.add)
+            if T in V_TGT:
+                nc.vector.tensor_tensor(out=y[:], in0=tg[T][:], in1=b2b[:], op=ALU.add)
+            else:
+                for h in range(2):
+                    nc.scalar.copy(out=y[:, 512 * h : 512 * (h + 1)], in_=tp[T, h][:])
             tb[T] = y
 
         def resid(T):
             y = sb.tile([P, D], F32, name="us", tag="us", bufs=2, align_bytes=64)
-            a = []
             for h in range(2):
                 s = sb.tile([P, 1], F32, name="sum", tag="sum" + str(h), bufs=2)
                 nc.vector.scalar_tensor_tensor(
                     out=y[:, 512 * h : 512 * (h + 1)], in0=acc[T, h][:], scalar=0.0,
                     in1=tb[T][:, 512 * h : 512 * (h + 1)], op0=ALU.add, op1=ALU.add, accum_out=s[:],
                 )
-                a.append(s)
-            m = sb.tile([P, 1], F32, name="nm", tag="nm", bufs=2)
+                sm[T, h] = s
+            us[T] = y
+
+        def negmean(T):
+            m = sb.tile([P, 1], F32, name="nm", tag="nm", bufs=3)
             nc.vector.tensor_scalar(
-                out=m[:], in0=a[0][:], scalar1=a[1][:], scalar2=-1.0 / D, op0=ALU.add, op1=ALU.mult
+                out=m[:], in0=sm[T, 0][:], scalar1=sm[T, 1][:], scalar2=-1.0 / D, op0=ALU.add, op1=ALU.mult
             )
-            us[T], st[T] = y, m
+            nm[T] = m
 
         def square(T):
             junk = sb.tile([P, D], F32, name="junk", tag="junk", bufs=1)
             ss = sb.tile([P, 1], F32, name="ss", tag="ss", bufs=2)
-            nc.scalar.activation(out=junk[:], in_=us[T][:], func=ACT.Square, bias=st[T][:], accum_out=ss[:])
-            sd = sb.tile([P, 1], F32, name="sd", tag="sd", bufs=2)
-            nc.scalar.activation(out=sd[:], in_=ss[:], func=ACT.Sqrt, scale=1.0 / D, bias=EPS)
-            st[T] = (st[T], sd)
+            nc.scalar.activation(out=junk[:], in_=us[T][:], func=ACT.Square, bias=nm[T][:], accum_out=ss[:])
+            s = sb.tile([P, 1], F32, name="sd", tag="sd", bufs=2)
+            nc.scalar.activation(out=s[:], in_=ss[:], func=ACT.Sqrt, scale=1.0 / D, bias=EPS)
+            sd[T] = s
+
+        def recip(T):
+            r = sb.tile([P, 1], F32, name="rs", tag="rs", bufs=2)
+            nc.vector.reciprocal(out=r[:], in_=sd[T][:])
+            rs[T] = r
 
         def norm(T):
-            m, sd = st[T]
-            r = sb.tile([P, 1], F32, name="rs", tag="rs", bufs=2)
-            nc.vector.reciprocal(out=r[:], in_=sd[:])
             y = sb.tile([P, D], F32, name="zs", tag="zs", bufs=2, align_bytes=64)
             nc.vector.tensor_scalar(
-                out=y[:], in0=us[T][:], scalar1=m[:], scalar2=r[:], op0=ALU.add, op1=ALU.mult
+                out=y[:], in0=us[T][:], scalar1=nm[T][:], scalar2=rs[T][:], op0=ALU.add, op1=ALU.mult
             )
             zs[T] = y
 
@@ -242,8 +287,8 @@ def tile_mldecoder_pb_w4_kernel(
                     for g in range(2):
                         nc.tensor.matmul_mx(
                             out=a[:, P * j : P * (j + 1)],
-                            lhsT=dc[T, g][:, P * kl : P * (kl + 1)].bitcast(FP8X4),
-                            lhsT_scale=ds[T, g][:, P * kl : P * (kl + 1)],
+                            lhsT=dc[2 * T + g][:, P * kl : P * (kl + 1)].bitcast(FP8X4),
+                            lhsT_scale=ds[2 * T + g][:, P * kl : P * (kl + 1)],
                             rhs=hc[T][:, P * g : P * (g + 1)].bitcast(FP8X4),
                             rhs_scale=hs[T][:, P * g : P * (g + 1)],
                             start=(g == 0),
@@ -273,51 +318,28 @@ def tile_mldecoder_pb_w4_kernel(
             nc.scalar.copy(out=y[:], in_=oT[T][:, 0:P])
             nc.scalar.dma_start(out=out_g[T], in_=y[:])
 
-        NU = 2 * NT
-        VW = {(2 * i + 1, 3) for i in range(0, NT)}
-        S_OF = [2 + (11 * T + 3) // 7 for T in range(NT)]
-        O_AT = {max(2 * T + 2, S_OF[T] + 2): T for T in range(NT)}
-        LN_AT = {S_OF[T]: T for T in range(NT)}
-
-        def load_unit(n):
-            load_dup(n // 2, n % 2)
-
-        def wid(n, ts):
-            if n < NU:
-                for t in ts:
-                    if (n, t) not in VW:
-                        widen("S", n // 2, n % 2, t)
-
-        def widv(n):
-            if n < NU:
-                for t in range(4):
-                    if (n, t) in VW:
-                        widen("V", n // 2, n % 2, t)
+        def at(n, f):
+            if n in LN_AT:
+                f(LN_AT[n])
 
         def out_at(n, f):
             if n in O_AT:
                 f(O_AT[n])
 
-        def at(n, f):
-            if n in LN_AT:
-                f(LN_AT[n])
-
-        load_unit(0)
         load_ff(0)
         load_unit(1)
         load_w2()
         load_w2s()
-        load_tgt(0)
         load_unit(2)
-        widen("S", 0, 0, 0)
-        widen("S", 0, 0, 2)
-        widen("V", 0, 0, 1)
-        widen("V", 0, 0, 3)
+        load_tgt(0)
+        wid(0, range(4))
+        widv(0)
         bp = psum.tile([P, 512], F32, name="so", tag="so", bufs=2)
         nc.vector.tensor_copy(out=browf[:], in_=brow[:])
         nc.tensor.transpose(bp[:, 0:P], browf[:], ident[:])
         nc.vector.tensor_copy(out=gf[:], in_=gb[:])
         nc.vector.tensor_copy(out=bf[:], in_=bb[:])
+        nc.vector.tensor_copy(out=identb[:], in_=ident[:])
         b2p = []
         for h in range(2):
             x = psum.tile([P, 512], F32, name="acc", tag="acc", bufs=2)
@@ -326,7 +348,6 @@ def tile_mldecoder_pb_w4_kernel(
         for h in range(2):
             nc.vector.tensor_copy(out=b2b[:, 512 * h : 512 * (h + 1)], in_=b2p[h][:])
         nc.vector.tensor_copy(out=biasT[:], in_=bp[:, 0:K])
-
         for n in range(NU):
             if n + 3 < NU:
                 load_unit(n + 3)
@@ -334,16 +355,20 @@ def tile_mldecoder_pb_w4_kernel(
                 load_ff(LN_AT[n + 4])
                 load_tgt(LN_AT[n + 4])
             at(n + 2, xpose_ff)
+            at(n - 1, recip)
+            at(n, resid)
             at(n - 1, norm)
             at(n - 1, xpose_z)
-            at(n, resid)
-            wid(n + 1, (0, 1))
+            at(n, negmean)
+            wid(n + 1, (0,))
             at(n + 1, quant_ff)
             at(n + 1, stage1)
             at(n + 2, evac_ff)
+            at(n + 1, tgt_mm)
+            wid(n + 1, (1,))
             at(n, square)
             at(n - 1, evac_h)
-            inter_dup(n // 2, n % 2)
+            inter_dup(n)
             at(n - 2, inter_h)
             out_at(n - 1, evac_out)
             out_at(n - 1, xpose_out)
@@ -351,12 +376,12 @@ def tile_mldecoder_pb_w4_kernel(
             wid(n + 1, (2,))
             out_at(n - 1, copy_out)
             if n > 0:
-                quant_dup((n - 1) // 2, (n - 1) % 2)
+                quant_dup(n - 1)
             at(n - 2, quant_h)
             wid(n + 1, (3,))
             widv(n + 1)
             out_at(n, stage2)
-        quant_dup(NT - 1, 1)
+        quant_dup(NU - 1)
         stage2(NT - 1)
         evac_out(NT - 1)
         xpose_out(NT - 1)

@@ -22,10 +22,10 @@ NT = 8
 KL = 8
 NU = 2 * NT
 EPS = 1e-5
-S_OF = [2 + (11 * T + 3) // 7 for T in range(NT)]
+S_OF = [2,5,6,7,9,10,11,13]
 LN_AT = {S_OF[T]: T for T in range(NT)}
 O_AT = {max(2 * T + 2, S_OF[T] + 2): T for T in range(NT)}
-V_TGT = (0, 1)
+EARLY = 3
 
 
 def tile_mldecoder_pb_w4_kernel(
@@ -49,51 +49,59 @@ def tile_mldecoder_pb_w4_kernel(
         so, res, oT = {}, {}, {}
 
         def load_unit(n, parts=1):
+            if n >= EARLY:
+                for t in range(4):
+                    r = sb.tile([P, KL * G], U8, name="rawt", tag="rawt", bufs=16, align_bytes=64)
+                    nc.sync.dma_start(
+                        out=r[:].rearrange("p (kl n) -> p kl n", kl=KL),
+                        in_=dup_g[n // 2][n % 2][:, :, G * t : G * (t + 1)],
+                    )
+                    raw[n, t] = r
+                return
             w = KL // parts
             for q in range(parts):
-                r = sb.tile([P, w * 4 * G], U8, name="raw", tag="raw" + str(parts), bufs=6 if parts == 1 else parts, align_bytes=64)
+                r = sb.tile([P, w * 4 * G], U8, name="raw", tag="raw" + str(n), bufs=parts, align_bytes=64)
                 nc.sync.dma_start(
                     out=r[:].rearrange("p (kl x) -> p kl x", kl=w), in_=dup_g[n // 2][n % 2][:, w * q : w * (q + 1), :]
                 )
                 for j in range(w):
-                    raw[n, w * q + j] = (r, j)
+                    raw[n, "kl", w * q + j] = (r, j)
 
         def load_ff(T):
-            x = sb.tile([P, FF], BF16, name="xf", tag="xf", bufs=3, align_bytes=64)
+            x = sb.tile([P, FF], BF16, name="xf", tag="xf", bufs=4, align_bytes=64)
             nc.sync.dma_start(out=x[:], in_=ff_g[T])
             xf[T] = x
 
         def load_tgt(T):
-            x = sb.tile([P, D], BF16, name="tg", tag="tg", bufs=3, align_bytes=64)
+            x = sb.tile([P, D], BF16, name="tg", tag="tg", bufs=4, align_bytes=64)
             nc.sync.dma_start(out=x[:], in_=tgt_g[T])
             tg[T] = x
 
-        dsc = keep.tile([P, 2, 4], F32, name="dsc")
-        nc.sync.dma_start(out=dsc[:], in_=dup_pool_scale.rearrange("o (g p t) u -> p (o g) (t u)", g=2, t=4))
-        load_unit(0, 4)
-        b2r = keep.tile([P, D], BF16, name="b2r", align_bytes=64)
-        nc.vector.memset(b2r[:], 0.0)
-        nc.gpsimd.dma_start(out=b2r[0:1, :], in_=b2.unsqueeze(0))
-        gb = keep.tile([P, 2, 4], BF16, name="gb")
-        bb = keep.tile([P, 2, 4], BF16, name="bb")
-        nc.gpsimd.dma_start(out=gb[:], in_=g3.rearrange("(g p t) -> p g t", g=2, t=4))
-        nc.gpsimd.dma_start(out=bb[:], in_=be3.rearrange("(g p t) -> p g t", g=2, t=4))
         ident = keep.tile([P, P], F32, name="ident")
         make_identity(nc, ident[:])
-        brow = keep.tile([P, P], BF16, name="brow", align_bytes=64)
-        nc.gpsimd.memset(brow[:], 0.0)
-        nc.gpsimd.dma_start(out=brow[0:K, :], in_=dup_bias.rearrange("(k g) -> k g", g=G))
-        ones = keep.tile([P, P], BF16, name="ones")
+        ones = keep.tile([P, 1], BF16, name="ones")
         nc.vector.memset(ones[:], 1.0)
         warm = keep.tile([P, 1], F32, name="warm")
         nc.scalar.activation(out=warm[:], in_=ones[:, 0:1], func=ACT.Sqrt)
+        brow = keep.tile([P, P], BF16, name="brow", align_bytes=64)
+        nc.vector.memset(brow[:], 0.0)
+        nc.gpsimd.dma_start(out=brow[K : K + 8, :], in_=b2.rearrange("(c n) -> c n", n=P))
+        nc.gpsimd.dma_start(out=brow[0:K, :], in_=dup_bias.rearrange("(k g) -> k g", g=G))
+        dsc = keep.tile([P, 2, 4], F32, name="dsc")
+        nc.sync.dma_start(out=dsc[:], in_=dup_pool_scale.rearrange("o (g p t) u -> p (o g) (t u)", g=2, t=4))
+        load_unit(0, 2)
+        load_ff(0)
+        load_unit(1)
+        gb = keep.tile([P, 2, 4], BF16, name="gb")
+        bb = keep.tile([P, 2, 4], BF16, name="bb")
+        nc.scalar.dma_start(out=gb[:], in_=g3.rearrange("(g p t) -> p g t", g=2, t=4))
+        nc.scalar.dma_start(out=bb[:], in_=be3.rearrange("(g p t) -> p g t", g=2, t=4))
         w2w = keep.tile([P, 4, 2 * D], U8, name="w2w", align_bytes=64)
         w2s = keep.tile([P, 4, D], U8, name="w2s", align_bytes=64)
         nc.vector.memset(w2s[:].rearrange("p g n -> p (g n)").bitcast(I32), 0)
         gf = keep.tile([P, 2, 4], F32, name="gf")
         bf = keep.tile([P, 2, 4], F32, name="bf")
-        biasT = keep.tile([P, K], F32, name="biasT")
-        b2b = keep.tile([P, D], F32, name="b2b")
+        biasT = keep.tile([P, P], F32, name="biasT")
         browf = keep.tile([P, P], F32, name="browf")
         identb = keep.tile([P, P], BF16, name="identb")
 
@@ -108,45 +116,69 @@ def tile_mldecoder_pb_w4_kernel(
                 )
 
         def vk(n):
-            return 4 if n < 2 else 1 + n % 2
+            return 4 if n < 2 else 2
+
+        def vt(n):
+            return [0,0,0,1,1,1,0,2,0,2,0,2,0,0,0,1][n]
 
         def widen(eng, n, t, kls):
             if n not in wd:
                 wd[n] = sb.tile([P, 4, KL * G], BF16, name="wd", tag="wd", bufs=3, align_bytes=64)
-            for kl in kls:
-                r, j = raw[n, kl]
-                lo = (4 * j + t) * G
-                src = r[:, lo : lo + G].bitcast(FP8)
-                dst = wd[n][:, t, kl * G : (kl + 1) * G]
-                scale = dsc[:, n % 2, t : t + 1]
+            scale = dsc[:, n % 2, t : t + 1]
+            pairs = [(raw[n, t][:], wd[n][:, t, :])] if n >= EARLY else [
+                (raw[n, "kl", kl][0][:, (4 * raw[n, "kl", kl][1] + t) * G : (4 * raw[n, "kl", kl][1] + t + 1) * G],
+                 wd[n][:, t, kl * G : (kl + 1) * G]) for kl in kls
+            ]
+            for src, dst in pairs:
                 if eng == "S":
-                    nc.scalar.activation(out=dst, in_=src, func=ACT.Copy, scale=scale)
+                    nc.scalar.activation(out=dst, in_=src.bitcast(FP8), func=ACT.Copy, scale=scale)
                 else:
-                    nc.vector.tensor_scalar(out=dst, in0=src, scalar1=scale, scalar2=None, op0=ALU.mult)
+                    nc.vector.tensor_scalar(out=dst, in0=src.bitcast(FP8), scalar1=scale, scalar2=None, op0=ALU.mult)
 
         def wid(n, ts):
             if n < NU:
                 for t in ts:
-                    widen("S", n, t, range(KL - vk(n)))
+                    if n < EARLY:
+                        widen("S", n, t, range(KL - vk(n)))
+                    elif t < 4 - vt(n):
+                        widen("S", n, t, ())
 
         def widv(n):
             if n < NU:
                 for t in range(4):
-                    widen("V", n, t, range(KL - vk(n), KL))
+                    if n < EARLY:
+                        widen("V", n, t, range(KL - vk(n), KL))
+                    elif t >= 4 - vt(n):
+                        widen("V", n, t, ())
+
+        def si(n):
+            return [1,0,0,0,0,0,0,0,0,0,0,0,0,0,0,4][n]
+
+        def inter_part(eng, n, k0, k1):
+            if n not in gd:
+                gd[n] = sb.tile([P, KL * G * 4], BF16, name="gd", tag="gd", bufs=3, align_bytes=64)
+            if k0 < k1:
+                dst = gd[n][:, 4 * G * k0 : 4 * G * k1].rearrange("p (c i t) -> p c t i", i=4, t=4)
+                src = wd[n][:, :, G * k0 : G * k1].rearrange("p t (c i) -> p c t i", i=4)
+                if eng == "S":
+                    nc.scalar.copy(out=dst, in_=src)
+                else:
+                    nc.vector.tensor_copy(out=dst, in_=src)
 
         def inter_dup(n):
-            y = sb.tile([P, KL * G * 4], BF16, name="gd", tag="gd", bufs=3, align_bytes=64)
-            nc.vector.tensor_copy(
-                out=y[:].rearrange("p (c i t) -> p c t i", i=4, t=4),
-                in_=wd[n][:].rearrange("p t (c i) -> p c t i", i=4),
-            )
-            gd[n] = y
+            inter_part("V", n, 0, KL - si(n))
 
-        def quant_dup(n):
-            c = sb.tile([P, KL * G], U32, name="dc", tag="dc", bufs=8, align_bytes=64)
-            s = sb.tile([P, KL * G], U8, name="ds", tag="ds", bufs=8, align_bytes=64)
-            nc.vector.quantize_mx(out=c[:].bitcast(FP8X4), scales=s[:], in_=gd[n][:])
-            dc[n], ds[n] = c, s
+        def inter_s(n):
+            inter_part("S", n, KL - si(n), KL)
+
+        def quant_dup(n, halves=(0, 2)):
+            if n not in dc:
+                dc[n] = sb.tile([P, KL * G], U32, name="dc", tag="dc", bufs=8, align_bytes=64)
+                ds[n] = sb.tile([P, KL * G], U8, name="ds", tag="ds", bufs=8, align_bytes=64)
+            lo, hi = halves[0] * 512, halves[1] * 512
+            nc.vector.quantize_mx(
+                out=dc[n][:, lo:hi].bitcast(FP8X4), scales=ds[n][:, lo:hi], in_=gd[n][:, 4 * lo : 4 * hi]
+            )
 
         def xpose_ff(T):
             words = xf[T][:].bitcast(F32)
@@ -191,21 +223,24 @@ def tile_mldecoder_pb_w4_kernel(
                 acc[T, h] = a
 
         def tgt_mm(T):
-            if T not in V_TGT:
-                for h in range(2):
-                    x = psum.tile([P, 512], F32, name="xt", tag="xt", bufs=2)
-                    cols = slice(512 * h, 512 * (h + 1))
-                    nc.tensor.matmul(x[:], lhsT=identb[:], rhs=tg[T][:, cols], start=True, stop=False)
-                    nc.tensor.matmul(x[:], lhsT=ones[:], rhs=b2r[:, cols], start=False, stop=True)
-                    tp[T, h] = x
+            for h in range(2):
+                x = psum.tile([P, 512], F32, name="xt", tag="xt", bufs=2)
+                nc.tensor.matmul(x[:], lhsT=identb[:], rhs=tg[T][:, 512 * h : 512 * (h + 1)], start=True, stop=False)
+                for c in range(4):
+                    col = K + 4 * h + c
+                    nc.tensor.matmul(
+                        x[:, P * c : P * (c + 1)], lhsT=biasT[:, col : col + 1].to_broadcast([P, P]), rhs=ident[:],
+                        is_transpose=True, start=False, stop=(c == 3),
+                    )
+                tp[T, h] = x
 
         def tgtb(T):
             y = sb.tile([P, D], F32, name="tb", tag="tb", bufs=2, align_bytes=64)
-            if T in V_TGT:
-                nc.vector.tensor_tensor(out=y[:], in0=tg[T][:], in1=b2b[:], op=ALU.add)
-            else:
-                for h in range(2):
-                    nc.scalar.copy(out=y[:, 512 * h : 512 * (h + 1)], in_=tp[T, h][:])
+            for h in range(2):
+                nc.scalar.copy(
+                    out=y[:, 512 * h : 512 * (h + 1)].rearrange("p (t q) -> p t q", t=4),
+                    in_=tp[T, h][:].rearrange("p (q t) -> p t q", t=4),
+                )
             tb[T] = y
 
         def resid(T):
@@ -213,8 +248,9 @@ def tile_mldecoder_pb_w4_kernel(
             for h in range(2):
                 s = sb.tile([P, 1], F32, name="sum", tag="sum" + str(h), bufs=2)
                 nc.vector.scalar_tensor_tensor(
-                    out=y[:, 512 * h : 512 * (h + 1)], in0=acc[T, h][:], scalar=0.0,
-                    in1=tb[T][:, 512 * h : 512 * (h + 1)], op0=ALU.add, op1=ALU.add, accum_out=s[:],
+                    out=y[:, 512 * h : 512 * (h + 1)].rearrange("p (t q) -> p t q", t=4),
+                    in0=acc[T, h][:].rearrange("p (q t) -> p t q", t=4), scalar=0.0,
+                    in1=tb[T][:, 512 * h : 512 * (h + 1)].rearrange("p (t q) -> p t q", t=4), op0=ALU.add, op1=ALU.add, accum_out=s[:],
                 )
                 sm[T, h] = s
             us[T] = y
@@ -250,8 +286,8 @@ def tile_mldecoder_pb_w4_kernel(
             for g in range(2):
                 x = psum.tile([P, 512], F32, name="ht", tag="ht", bufs=2)
                 for t in range(4):
-                    lo = 512 * g + t
-                    nc.tensor.transpose(x[:, P * t : P * (t + 1)], zs[T][:, lo : lo + 509 : 4], ident[:])
+                    lo = 512 * g + P * t
+                    nc.tensor.transpose(x[:, P * t : P * (t + 1)], zs[T][:, lo : lo + P], ident[:])
                 ht[T, g] = x
 
         def evac_h(T):
@@ -279,8 +315,8 @@ def tile_mldecoder_pb_w4_kernel(
             nc.vector.quantize_mx(out=c[:].bitcast(FP8X4), scales=s[:], in_=hg[T][:])
             hc[T], hs[T] = c, s
 
-        def stage2(T):
-            for h in range(2):
+        def stage2(T, hs_=(0, 1)):
+            for h in hs_:
                 a = psum.tile([P, 512], F32, name="so", tag="so", bufs=2)
                 for j in range(4):
                     kl = 4 * h + j
@@ -299,7 +335,7 @@ def tile_mldecoder_pb_w4_kernel(
         def evac_out(T):
             y = sb.tile([P, P], F32, name="res", tag="res", bufs=2, align_bytes=64)
             yv = y[:].rearrange("p (b kl) -> p kl b", kl=KL)
-            bv = biasT[:].rearrange("p (kl kt) -> p kl kt", kt=NT)
+            bv = biasT[:, 0:K].rearrange("p (kl kt) -> p kl kt", kt=NT)
             for h in range(2):
                 v = so[T, h][:, 64 * h : 64 * h + 448].rearrange("p (a c) -> p a c", c=16)[:, 0:28:9, :]
                 nc.vector.tensor_tensor(
@@ -318,6 +354,17 @@ def tile_mldecoder_pb_w4_kernel(
             nc.scalar.copy(out=y[:], in_=oT[T][:, 0:P])
             nc.scalar.dma_start(out=out_g[T], in_=y[:])
 
+        def consts_b2():
+            nc.vector.tensor_copy(out=browf[:], in_=brow[:])
+            nc.vector.tensor_copy(out=identb[:], in_=ident[:])
+            x = psum.tile([P, 512], F32, name="so", tag="so", bufs=2)
+            nc.tensor.transpose(x[:, 0:P], browf[:], ident[:])
+            nc.vector.tensor_copy(out=biasT[:], in_=x[:, 0:P])
+
+        def consts_rest():
+            nc.vector.tensor_copy(out=gf[:], in_=gb[:])
+            nc.vector.tensor_copy(out=bf[:], in_=bb[:])
+
         def at(n, f):
             if n in LN_AT:
                 f(LN_AT[n])
@@ -326,63 +373,54 @@ def tile_mldecoder_pb_w4_kernel(
             if n in O_AT:
                 f(O_AT[n])
 
-        load_ff(0)
-        load_unit(1)
         load_w2()
         load_w2s()
         load_unit(2)
         load_tgt(0)
         wid(0, range(4))
         widv(0)
-        bp = psum.tile([P, 512], F32, name="so", tag="so", bufs=2)
-        nc.vector.tensor_copy(out=browf[:], in_=brow[:])
-        nc.tensor.transpose(bp[:, 0:P], browf[:], ident[:])
-        nc.vector.tensor_copy(out=gf[:], in_=gb[:])
-        nc.vector.tensor_copy(out=bf[:], in_=bb[:])
-        nc.vector.tensor_copy(out=identb[:], in_=ident[:])
-        b2p = []
-        for h in range(2):
-            x = psum.tile([P, 512], F32, name="acc", tag="acc", bufs=2)
-            nc.tensor.matmul(x[:], lhsT=ones[:], rhs=b2r[:, 512 * h : 512 * (h + 1)], start=True, stop=True)
-            b2p.append(x)
-        for h in range(2):
-            nc.vector.tensor_copy(out=b2b[:, 512 * h : 512 * (h + 1)], in_=b2p[h][:])
-        nc.vector.tensor_copy(out=biasT[:], in_=bp[:, 0:K])
         for n in range(NU):
             if n + 3 < NU:
                 load_unit(n + 3)
             if n + 4 in LN_AT and LN_AT[n + 4] > 0:
                 load_ff(LN_AT[n + 4])
                 load_tgt(LN_AT[n + 4])
-            at(n + 2, xpose_ff)
             at(n - 1, recip)
-            at(n, resid)
-            at(n - 1, norm)
-            at(n - 1, xpose_z)
-            at(n, negmean)
-            wid(n + 1, (0,))
-            at(n + 1, quant_ff)
-            at(n + 1, stage1)
-            at(n + 2, evac_ff)
-            at(n + 1, tgt_mm)
-            wid(n + 1, (1,))
-            at(n, square)
-            at(n - 1, evac_h)
-            inter_dup(n)
-            at(n - 2, inter_h)
-            out_at(n - 1, evac_out)
-            out_at(n - 1, xpose_out)
-            at(n + 1, tgtb)
+            at(n + 2, xpose_ff)
             wid(n + 1, (2,))
-            out_at(n - 1, copy_out)
+            at(n - 2, inter_h)
+            at(n + 1, quant_ff)
+            at(n - 1, norm)
+            if n == 2:
+                consts_rest()
+            if n == 0:
+                consts_b2()
+            at(n, resid)
             if n > 0:
                 quant_dup(n - 1)
-            at(n - 2, quant_h)
-            wid(n + 1, (3,))
+            wid(n + 1, (0,))
+            at(n, negmean)
+            at(n - 1, xpose_z)
+            inter_s(n)
             widv(n + 1)
+            at(n - 1, evac_h)
+            out_at(n - 1, evac_out)
+            at(n + 2, evac_ff)
+            at(n + 1, stage1)
+            out_at(n - 1, xpose_out)
+            at(n, square)
+            wid(n + 1, (1,))
+            inter_dup(n)
+            at(n + 1, tgt_mm)
+            at(n + 1, tgtb)
+            out_at(n - 1, copy_out)
+            wid(n + 1, (3,))
+            at(n - 2, quant_h)
             out_at(n, stage2)
-        quant_dup(NU - 1)
-        stage2(NT - 1)
+        quant_dup(NU - 1, (0, 1))
+        stage2(NT - 1, (0,))
+        quant_dup(NU - 1, (1, 2))
+        stage2(NT - 1, (1,))
         evac_out(NT - 1)
         xpose_out(NT - 1)
         copy_out(NT - 1)

@@ -22,10 +22,12 @@ NT = 8
 KL = 8
 NU = 2 * NT
 EPS = 1e-5
-S_OF = [2,5,6,7,9,10,11,13]
+S_OF = [2,5,6,7,8,9,11,12]
 LN_AT = {S_OF[T]: T for T in range(NT)}
 O_AT = {max(2 * T + 2, S_OF[T] + 2): T for T in range(NT)}
 EARLY = 3
+V_PLANES = [6,4,6,1,3,1,0,2,0,3,1,0,1,2,0,0]
+S_KLS = [1,2,0,1,2,0,0,0,2,0,0,0,1,1,1,4]
 
 
 def tile_mldecoder_pb_w4_kernel(
@@ -49,40 +51,37 @@ def tile_mldecoder_pb_w4_kernel(
         so, res, oT = {}, {}, {}
 
         def load_unit(n, parts=1):
-            if n >= EARLY:
+            src = dup_g[n // 2][n % 2]
+            if n < EARLY:
+                w = KL // parts
+                for q in range(parts):
+                    r = sb.tile([P, w * 4 * G], U8, name="raw", tag="raw" + str(parts), bufs=max(parts, EARLY - 1), align_bytes=64)
+                    nc.sync.dma_start(out=r[:].rearrange("p (kl x) -> p kl x", kl=w), in_=src[:, w * q : w * (q + 1), :])
+                    for j in range(w):
+                        for t in range(4):
+                            raw[n, t, w * q + j] = r[:, G * (4 * j + t) : G * (4 * j + t + 1)]
+            else:
                 for t in range(4):
                     r = sb.tile([P, KL * G], U8, name="rawt", tag="rawt", bufs=16, align_bytes=64)
                     nc.sync.dma_start(
-                        out=r[:].rearrange("p (kl n) -> p kl n", kl=KL),
-                        in_=dup_g[n // 2][n % 2][:, :, G * t : G * (t + 1)],
+                        out=r[:].rearrange("p (kl n) -> p kl n", kl=KL), in_=src[:, :, G * t : G * (t + 1)]
                     )
-                    raw[n, t] = r
-                return
-            w = KL // parts
-            for q in range(parts):
-                r = sb.tile([P, w * 4 * G], U8, name="raw", tag="raw" + str(n), bufs=parts, align_bytes=64)
-                nc.sync.dma_start(
-                    out=r[:].rearrange("p (kl x) -> p kl x", kl=w), in_=dup_g[n // 2][n % 2][:, w * q : w * (q + 1), :]
-                )
-                for j in range(w):
-                    raw[n, "kl", w * q + j] = (r, j)
+                    raw[n, t] = r[:]
 
         def load_ff(T):
-            x = sb.tile([P, FF], BF16, name="xf", tag="xf", bufs=4, align_bytes=64)
-            nc.sync.dma_start(out=x[:], in_=ff_g[T])
-            xf[T] = x
+            xf[T] = sb.tile([P, FF], BF16, name="xf", tag="xf", bufs=4, align_bytes=64)
+            nc.sync.dma_start(out=xf[T][:], in_=ff_g[T])
 
         def load_tgt(T):
-            x = sb.tile([P, D], BF16, name="tg", tag="tg", bufs=4, align_bytes=64)
-            nc.sync.dma_start(out=x[:], in_=tgt_g[T])
-            tg[T] = x
+            tg[T] = sb.tile([P, D], BF16, name="tg", tag="tg", bufs=4, align_bytes=64)
+            nc.sync.dma_start(out=tg[T][:], in_=tgt_g[T])
 
         ident = keep.tile([P, P], F32, name="ident")
         make_identity(nc, ident[:])
         ones = keep.tile([P, 1], BF16, name="ones")
         nc.vector.memset(ones[:], 1.0)
         warm = keep.tile([P, 1], F32, name="warm")
-        nc.scalar.activation(out=warm[:], in_=ones[:, 0:1], func=ACT.Sqrt)
+        nc.scalar.activation(out=warm[:], in_=ones[:], func=ACT.Sqrt)
         brow = keep.tile([P, P], BF16, name="brow", align_bytes=64)
         nc.vector.memset(brow[:], 0.0)
         nc.gpsimd.dma_start(out=brow[K : K + 8, :], in_=b2.rearrange("(c n) -> c n", n=P))
@@ -101,62 +100,60 @@ def tile_mldecoder_pb_w4_kernel(
         nc.vector.memset(w2s[:].rearrange("p g n -> p (g n)").bitcast(I32), 0)
         gf = keep.tile([P, 2, 4], F32, name="gf")
         bf = keep.tile([P, 2, 4], F32, name="bf")
-        biasT = keep.tile([P, P], F32, name="biasT")
+        cols = keep.tile([P, P], F32, name="cols")
         browf = keep.tile([P, P], F32, name="browf")
         identb = keep.tile([P, P], BF16, name="identb")
 
         def load_w2():
             nc.sync.dma_start(out=w2w[:], in_=w2_words.rearrange("g p n -> p g n"))
-
-        def load_w2s():
-            for Q in range(4):
+            for q in range(4):
                 nc.sync.dma_start(
-                    out=w2s[32 * Q : 32 * Q + 4, :, :].bitcast(I32),
-                    in_=w2_scales[:, 4 * Q : 4 * Q + 4, :].rearrange("g q n -> q g n").bitcast(I32),
+                    out=w2s[32 * q : 32 * q + 4, :, :].bitcast(I32),
+                    in_=w2_scales[:, 4 * q : 4 * q + 4, :].rearrange("g q n -> q g n").bitcast(I32),
                 )
 
-        def vk(n):
-            return 4 if n < 2 else 2
+        def consts_early():
+            nc.vector.tensor_copy(out=browf[:], in_=brow[:])
+            nc.vector.tensor_copy(out=identb[:], in_=ident[:])
+            x = psum.tile([P, 512], F32, name="so", tag="so", bufs=2)
+            nc.tensor.transpose(x[:, 0:P], browf[:], ident[:])
+            nc.vector.tensor_copy(out=cols[:], in_=x[:, 0:P])
 
-        def vt(n):
-            return [0,0,0,1,1,1,0,2,0,2,0,2,0,0,0,1][n]
+        def consts_late():
+            nc.vector.tensor_copy(out=gf[:], in_=gb[:])
+            nc.vector.tensor_copy(out=bf[:], in_=bb[:])
 
-        def widen(eng, n, t, kls):
+        def widen(eng, n, t, dst_cols, src):
             if n not in wd:
                 wd[n] = sb.tile([P, 4, KL * G], BF16, name="wd", tag="wd", bufs=3, align_bytes=64)
+            dst = wd[n][:, t, dst_cols]
             scale = dsc[:, n % 2, t : t + 1]
-            pairs = [(raw[n, t][:], wd[n][:, t, :])] if n >= EARLY else [
-                (raw[n, "kl", kl][0][:, (4 * raw[n, "kl", kl][1] + t) * G : (4 * raw[n, "kl", kl][1] + t + 1) * G],
-                 wd[n][:, t, kl * G : (kl + 1) * G]) for kl in kls
-            ]
-            for src, dst in pairs:
-                if eng == "S":
-                    nc.scalar.activation(out=dst, in_=src.bitcast(FP8), func=ACT.Copy, scale=scale)
-                else:
-                    nc.vector.tensor_scalar(out=dst, in0=src.bitcast(FP8), scalar1=scale, scalar2=None, op0=ALU.mult)
+            if eng == "S":
+                nc.scalar.activation(out=dst, in_=src.bitcast(FP8), func=ACT.Copy, scale=scale)
+            else:
+                nc.vector.tensor_scalar(out=dst, in0=src.bitcast(FP8), scalar1=scale, scalar2=None, op0=ALU.mult)
 
-        def wid(n, ts):
-            if n < NU:
-                for t in ts:
-                    if n < EARLY:
-                        widen("S", n, t, range(KL - vk(n)))
-                    elif t < 4 - vt(n):
-                        widen("S", n, t, ())
+        def widen_part(eng, n, t):
+            if n >= NU:
+                return
+            if n < EARLY:
+                vk = V_PLANES[n]
+                for kl in (range(0, KL - vk) if eng == "S" else range(KL - vk, KL)):
+                    widen(eng, n, t, slice(G * kl, G * (kl + 1)), raw[n, t, kl])
+            elif (eng == "V") == (t >= 4 - V_PLANES[n]):
+                widen(eng, n, t, slice(0, KL * G), raw[n, t])
+
+        def wid(n, t):
+            widen_part("S", n, t)
 
         def widv(n):
-            if n < NU:
-                for t in range(4):
-                    if n < EARLY:
-                        widen("V", n, t, range(KL - vk(n), KL))
-                    elif t >= 4 - vt(n):
-                        widen("V", n, t, ())
+            for t in range(4):
+                widen_part("V", n, t)
 
-        def si(n):
-            return [1,0,0,0,0,0,0,0,0,0,0,0,0,0,0,4][n]
-
-        def inter_part(eng, n, k0, k1):
+        def inter(eng, n):
             if n not in gd:
                 gd[n] = sb.tile([P, KL * G * 4], BF16, name="gd", tag="gd", bufs=3, align_bytes=64)
+            k0, k1 = (0, KL - S_KLS[n]) if eng == "V" else (KL - S_KLS[n], KL)
             if k0 < k1:
                 dst = gd[n][:, 4 * G * k0 : 4 * G * k1].rearrange("p (c i t) -> p c t i", i=4, t=4)
                 src = wd[n][:, :, G * k0 : G * k1].rearrange("p t (c i) -> p c t i", i=4)
@@ -165,219 +162,178 @@ def tile_mldecoder_pb_w4_kernel(
                 else:
                     nc.vector.tensor_copy(out=dst, in_=src)
 
-        def inter_dup(n):
-            inter_part("V", n, 0, KL - si(n))
-
-        def inter_s(n):
-            inter_part("S", n, KL - si(n), KL)
-
-        def quant_dup(n, halves=(0, 2)):
+        def quant_dup(n, lo=0, hi=KL * G):
             if n not in dc:
                 dc[n] = sb.tile([P, KL * G], U32, name="dc", tag="dc", bufs=8, align_bytes=64)
                 ds[n] = sb.tile([P, KL * G], U8, name="ds", tag="ds", bufs=8, align_bytes=64)
-            lo, hi = halves[0] * 512, halves[1] * 512
             nc.vector.quantize_mx(
                 out=dc[n][:, lo:hi].bitcast(FP8X4), scales=ds[n][:, lo:hi], in_=gd[n][:, 4 * lo : 4 * hi]
             )
 
-        def xpose_ff(T):
+        def xpose_ff(T, j):
             words = xf[T][:].bitcast(F32)
-            for j in range(2):
-                x = psum.tile([P, 512], F32, name="xt", tag="xt", bufs=2)
-                for gg in range(2):
-                    for u in range(2):
-                        lo = 256 * (2 * j + gg) + u
-                        nc.tensor.transpose(
-                            x[:, 256 * gg + 128 * u : 256 * gg + 128 * u + 128], words[:, lo : lo + 255 : 2], ident[:]
-                        )
-                xt[T, j] = x
+            xt[T, j] = psum.tile([P, 512], F32, name="xt", tag="xt", bufs=2)
+            for i in range(4):
+                lo = 256 * (2 * j + i // 2) + i % 2
+                nc.tensor.transpose(xt[T, j][:, P * i : P * (i + 1)], words[:, lo : lo + 255 : 2], ident[:])
 
-        def evac_ff(T):
-            y = sb.tile([P, 4 * P * 4], BF16, name="xg", tag="xg", bufs=2, align_bytes=64)
-            for j in range(2):
-                nc.scalar.copy(
-                    out=y[:, 1024 * j : 1024 * (j + 1)].bitcast(F32).rearrange("p (g r u) -> p g r u", g=2, u=2),
-                    in_=xt[T, j][:].rearrange("p (g u r) -> p g r u", g=2, u=2),
-                )
-            xg[T] = y
+        def evac_ff(T, j):
+            if T not in xg:
+                xg[T] = sb.tile([P, 4 * P * 4], BF16, name="xg", tag="xg", bufs=2, align_bytes=64)
+            nc.scalar.copy(
+                out=xg[T][:, 1024 * j : 1024 * (j + 1)].bitcast(F32).rearrange("p (g r u) -> p g r u", g=2, u=2),
+                in_=xt[T, j][:].rearrange("p (g u r) -> p g r u", g=2, u=2),
+            )
 
         def quant_ff(T):
-            c = sb.tile([P, 4 * P], U32, name="fc", tag="fc", bufs=2, align_bytes=64)
-            s = sb.tile([P, 4 * P], U8, name="fs", tag="fs", bufs=2, align_bytes=64)
-            nc.vector.quantize_mx(out=c[:].bitcast(FP8X4), scales=s[:], in_=xg[T][:])
-            fc[T], fs[T] = c, s
+            fc[T] = sb.tile([P, 4 * P], U32, name="fc", tag="fc", bufs=2, align_bytes=64)
+            fs[T] = sb.tile([P, 4 * P], U8, name="fs", tag="fs", bufs=2, align_bytes=64)
+            nc.vector.quantize_mx(out=fc[T][:].bitcast(FP8X4), scales=fs[T][:], in_=xg[T][:])
 
-        def stage1(T):
-            for h in range(2):
-                a = psum.tile([P, 512], F32, name="acc", tag="acc", bufs=2)
-                for g in range(4):
-                    nc.tensor.matmul_mx(
-                        out=a[:],
-                        lhsT=fc[T][:, P * g : P * (g + 1)].bitcast(FP8X4),
-                        lhsT_scale=fs[T][:, P * g : P * (g + 1)],
-                        rhs=w2w[:, g, 1024 * h : 1024 * (h + 1)].bitcast(FP4X4),
-                        rhs_scale=w2s[:, g, 512 * h : 512 * (h + 1)],
-                        start=(g == 0),
-                        stop=(g == 3),
-                    )
-                acc[T, h] = a
-
-        def tgt_mm(T):
-            for h in range(2):
-                x = psum.tile([P, 512], F32, name="xt", tag="xt", bufs=2)
-                nc.tensor.matmul(x[:], lhsT=identb[:], rhs=tg[T][:, 512 * h : 512 * (h + 1)], start=True, stop=False)
-                for c in range(4):
-                    col = K + 4 * h + c
-                    nc.tensor.matmul(
-                        x[:, P * c : P * (c + 1)], lhsT=biasT[:, col : col + 1].to_broadcast([P, P]), rhs=ident[:],
-                        is_transpose=True, start=False, stop=(c == 3),
-                    )
-                tp[T, h] = x
-
-        def tgtb(T):
-            y = sb.tile([P, D], F32, name="tb", tag="tb", bufs=2, align_bytes=64)
-            for h in range(2):
-                nc.scalar.copy(
-                    out=y[:, 512 * h : 512 * (h + 1)].rearrange("p (t q) -> p t q", t=4),
-                    in_=tp[T, h][:].rearrange("p (q t) -> p t q", t=4),
+        def stage1(T, part):
+            h = part // 2
+            if part % 2 == 0:
+                acc[T, h] = psum.tile([P, 512], F32, name="acc", tag="acc", bufs=2)
+            for g in (0, 1) if part % 2 == 0 else (2, 3):
+                nc.tensor.matmul_mx(
+                    out=acc[T, h][:],
+                    lhsT=fc[T][:, P * g : P * (g + 1)].bitcast(FP8X4),
+                    lhsT_scale=fs[T][:, P * g : P * (g + 1)],
+                    rhs=w2w[:, g, 1024 * h : 1024 * (h + 1)].bitcast(FP4X4),
+                    rhs_scale=w2s[:, g, 512 * h : 512 * (h + 1)],
+                    start=(g == 0),
+                    stop=(g == 3),
                 )
-            tb[T] = y
 
-        def resid(T):
-            y = sb.tile([P, D], F32, name="us", tag="us", bufs=2, align_bytes=64)
-            for h in range(2):
-                s = sb.tile([P, 1], F32, name="sum", tag="sum" + str(h), bufs=2)
-                nc.vector.scalar_tensor_tensor(
-                    out=y[:, 512 * h : 512 * (h + 1)].rearrange("p (t q) -> p t q", t=4),
-                    in0=acc[T, h][:].rearrange("p (q t) -> p t q", t=4), scalar=0.0,
-                    in1=tb[T][:, 512 * h : 512 * (h + 1)].rearrange("p (t q) -> p t q", t=4), op0=ALU.add, op1=ALU.add, accum_out=s[:],
+        def tgt_mm(T, h):
+            x = psum.tile([P, 512], F32, name="xt", tag="xt", bufs=2)
+            nc.tensor.matmul(x[:], lhsT=identb[:], rhs=tg[T][:, 512 * h : 512 * (h + 1)], start=True, stop=False)
+            for c in range(4):
+                col = K + 4 * h + c
+                nc.tensor.matmul(
+                    x[:, P * c : P * (c + 1)], lhsT=cols[:, col : col + 1].to_broadcast([P, P]), rhs=ident[:],
+                    is_transpose=True, start=False, stop=(c == 3),
                 )
-                sm[T, h] = s
-            us[T] = y
+            tp[T, h] = x
+
+        def tgtb(T, h):
+            if T not in tb:
+                tb[T] = sb.tile([P, D], F32, name="tb", tag="tb", bufs=2, align_bytes=64)
+            nc.scalar.copy(
+                out=tb[T][:, 512 * h : 512 * (h + 1)].rearrange("p (t q) -> p t q", t=4),
+                in_=tp[T, h][:].rearrange("p (q t) -> p t q", t=4),
+            )
+
+        def resid(T, h):
+            if T not in us:
+                us[T] = sb.tile([P, D], F32, name="us", tag="us", bufs=2, align_bytes=64)
+            half = slice(512 * h, 512 * (h + 1))
+            sm[T, h] = sb.tile([P, 1], F32, name="sum", tag="sum", bufs=4)
+            nc.vector.scalar_tensor_tensor(
+                out=us[T][:, half].rearrange("p (t q) -> p t q", t=4),
+                in0=acc[T, h][:].rearrange("p (q t) -> p t q", t=4), scalar=0.0,
+                in1=tb[T][:, half].rearrange("p (t q) -> p t q", t=4),
+                op0=ALU.add, op1=ALU.add, accum_out=sm[T, h][:],
+            )
 
         def negmean(T):
-            m = sb.tile([P, 1], F32, name="nm", tag="nm", bufs=3)
+            nm[T] = sb.tile([P, 1], F32, name="nm", tag="nm", bufs=3)
             nc.vector.tensor_scalar(
-                out=m[:], in0=sm[T, 0][:], scalar1=sm[T, 1][:], scalar2=-1.0 / D, op0=ALU.add, op1=ALU.mult
+                out=nm[T][:], in0=sm[T, 0][:], scalar1=sm[T, 1][:], scalar2=-1.0 / D, op0=ALU.add, op1=ALU.mult
             )
-            nm[T] = m
 
         def square(T):
             junk = sb.tile([P, D], F32, name="junk", tag="junk", bufs=1)
             ss = sb.tile([P, 1], F32, name="ss", tag="ss", bufs=2)
             nc.scalar.activation(out=junk[:], in_=us[T][:], func=ACT.Square, bias=nm[T][:], accum_out=ss[:])
-            s = sb.tile([P, 1], F32, name="sd", tag="sd", bufs=2)
-            nc.scalar.activation(out=s[:], in_=ss[:], func=ACT.Sqrt, scale=1.0 / D, bias=EPS)
-            sd[T] = s
+            sd[T] = sb.tile([P, 1], F32, name="sd", tag="sd", bufs=2)
+            nc.scalar.activation(out=sd[T][:], in_=ss[:], func=ACT.Sqrt, scale=1.0 / D, bias=EPS)
 
         def recip(T):
-            r = sb.tile([P, 1], F32, name="rs", tag="rs", bufs=2)
-            nc.vector.reciprocal(out=r[:], in_=sd[T][:])
-            rs[T] = r
+            rs[T] = sb.tile([P, 1], F32, name="rs", tag="rs", bufs=2)
+            nc.vector.reciprocal(out=rs[T][:], in_=sd[T][:])
 
         def norm(T):
-            y = sb.tile([P, D], F32, name="zs", tag="zs", bufs=2, align_bytes=64)
+            zs[T] = sb.tile([P, D], F32, name="zs", tag="zs", bufs=2, align_bytes=64)
             nc.vector.tensor_scalar(
-                out=y[:], in0=us[T][:], scalar1=nm[T][:], scalar2=rs[T][:], op0=ALU.add, op1=ALU.mult
+                out=zs[T][:], in0=us[T][:], scalar1=nm[T][:], scalar2=rs[T][:], op0=ALU.add, op1=ALU.mult
             )
-            zs[T] = y
 
-        def xpose_z(T):
-            for g in range(2):
-                x = psum.tile([P, 512], F32, name="ht", tag="ht", bufs=2)
-                for t in range(4):
-                    lo = 512 * g + P * t
-                    nc.tensor.transpose(x[:, P * t : P * (t + 1)], zs[T][:, lo : lo + P], ident[:])
-                ht[T, g] = x
+        def xpose_z(T, g):
+            ht[T, g] = psum.tile([P, 512], F32, name="ht", tag="ht", bufs=2)
+            for t in range(4):
+                lo = 512 * g + P * t
+                nc.tensor.transpose(ht[T, g][:, P * t : P * (t + 1)], zs[T][:, lo : lo + P], ident[:])
 
-        def evac_h(T):
-            y = sb.tile([P, 2, 4, P], BF16, name="hp", tag="hp", bufs=2, align_bytes=64)
-            for g in range(2):
-                for t in range(4):
-                    nc.scalar.activation(
-                        out=y[:, g, t, :], in_=ht[T, g][:, P * t : P * (t + 1)], func=ACT.Identity,
-                        scale=gf[:, g, t : t + 1], bias=bf[:, g, t : t + 1],
-                    )
-            hp[T] = y
+        def evac_h(T, g):
+            if T not in hp:
+                hp[T] = sb.tile([P, 2, 4, P], BF16, name="hp", tag="hp", bufs=2, align_bytes=64)
+            for t in range(4):
+                nc.scalar.activation(
+                    out=hp[T][:, g, t, :], in_=ht[T, g][:, P * t : P * (t + 1)], func=ACT.Identity,
+                    scale=gf[:, g, t : t + 1], bias=bf[:, g, t : t + 1],
+                )
 
         def inter_h(T):
-            y = sb.tile([P, 2 * P * 4], BF16, name="hg", tag="hg", bufs=2, align_bytes=64)
+            hg[T] = sb.tile([P, 2 * P * 4], BF16, name="hg", tag="hg", bufs=2, align_bytes=64)
             for g in range(2):
                 nc.vector.tensor_copy(
-                    out=y[:, 512 * g : 512 * (g + 1)].rearrange("p (kl b t) -> p kl b t", kl=KL, t=4),
+                    out=hg[T][:, 512 * g : 512 * (g + 1)].rearrange("p (kl b t) -> p kl b t", kl=KL, t=4),
                     in_=hp[T][:, g, :, :].rearrange("p t (b kl) -> p kl b t", kl=KL),
                 )
-            hg[T] = y
 
         def quant_h(T):
-            c = sb.tile([P, 2 * P], U32, name="hc", tag="hc", bufs=4, align_bytes=64)
-            s = sb.tile([P, 2 * P], U8, name="hs", tag="hs", bufs=4, align_bytes=64)
-            nc.vector.quantize_mx(out=c[:].bitcast(FP8X4), scales=s[:], in_=hg[T][:])
-            hc[T], hs[T] = c, s
+            hc[T] = sb.tile([P, 2 * P], U32, name="hc", tag="hc", bufs=4, align_bytes=64)
+            hs[T] = sb.tile([P, 2 * P], U8, name="hs", tag="hs", bufs=4, align_bytes=64)
+            nc.vector.quantize_mx(out=hc[T][:].bitcast(FP8X4), scales=hs[T][:], in_=hg[T][:])
 
-        def stage2(T, hs_=(0, 1)):
-            for h in hs_:
-                a = psum.tile([P, 512], F32, name="so", tag="so", bufs=2)
-                for j in range(4):
-                    kl = 4 * h + j
-                    for g in range(2):
-                        nc.tensor.matmul_mx(
-                            out=a[:, P * j : P * (j + 1)],
-                            lhsT=dc[2 * T + g][:, P * kl : P * (kl + 1)].bitcast(FP8X4),
-                            lhsT_scale=ds[2 * T + g][:, P * kl : P * (kl + 1)],
-                            rhs=hc[T][:, P * g : P * (g + 1)].bitcast(FP8X4),
-                            rhs_scale=hs[T][:, P * g : P * (g + 1)],
-                            start=(g == 0),
-                            stop=(g == 1),
-                        )
-                so[T, h] = a
+        def stage2(T, h):
+            so[T, h] = psum.tile([P, 512], F32, name="so", tag="so", bufs=2)
+            for j in range(4):
+                kl = 4 * h + j
+                for g in range(2):
+                    nc.tensor.matmul_mx(
+                        out=so[T, h][:, P * j : P * (j + 1)],
+                        lhsT=dc[2 * T + g][:, P * kl : P * (kl + 1)].bitcast(FP8X4),
+                        lhsT_scale=ds[2 * T + g][:, P * kl : P * (kl + 1)],
+                        rhs=hc[T][:, P * g : P * (g + 1)].bitcast(FP8X4),
+                        rhs_scale=hs[T][:, P * g : P * (g + 1)],
+                        start=(g == 0),
+                        stop=(g == 1),
+                    )
 
-        def evac_out(T):
-            y = sb.tile([P, P], F32, name="res", tag="res", bufs=2, align_bytes=64)
-            yv = y[:].rearrange("p (b kl) -> p kl b", kl=KL)
-            bv = biasT[:, 0:K].rearrange("p (kl kt) -> p kl kt", kt=NT)
-            for h in range(2):
-                v = so[T, h][:, 64 * h : 64 * h + 448].rearrange("p (a c) -> p a c", c=16)[:, 0:28:9, :]
-                nc.vector.tensor_tensor(
-                    out=yv[:, 4 * h : 4 * h + 4, :], in0=v,
-                    in1=bv[:, 4 * h : 4 * h + 4, T : T + 1].to_broadcast([P, 4, B]), op=ALU.add,
-                )
-            res[T] = y
+        def evac_out(T, h):
+            if T not in res:
+                res[T] = sb.tile([P, P], F32, name="res", tag="res", bufs=2, align_bytes=64)
+            v = so[T, h][:, 64 * h : 64 * h + 448].rearrange("p (a c) -> p a c", c=16)[:, 0:28:9, :]
+            bias = cols[:, 0:K].rearrange("p (kl kt) -> p kl kt", kt=NT)[:, 4 * h : 4 * h + 4, T : T + 1]
+            nc.vector.tensor_tensor(
+                out=res[T][:].rearrange("p (b kl) -> p kl b", kl=KL)[:, 4 * h : 4 * h + 4, :],
+                in0=v, in1=bias.to_broadcast([P, 4, B]), op=ALU.add,
+            )
 
         def xpose_out(T):
-            x = psum.tile([P, 512], F32, name="so", tag="so", bufs=2)
-            nc.tensor.transpose(x[:, 0:P], res[T][:], ident[:])
-            oT[T] = x
+            oT[T] = psum.tile([P, 512], F32, name="so", tag="so", bufs=2)
+            nc.tensor.transpose(oT[T][:, 0:P], res[T][:], ident[:])
 
         def copy_out(T):
             y = sb.tile([P, G], F32, name="ot", tag="ot", bufs=2, align_bytes=64)
             nc.scalar.copy(out=y[:], in_=oT[T][:, 0:P])
             nc.scalar.dma_start(out=out_g[T], in_=y[:])
 
-        def consts_b2():
-            nc.vector.tensor_copy(out=browf[:], in_=brow[:])
-            nc.vector.tensor_copy(out=identb[:], in_=ident[:])
-            x = psum.tile([P, 512], F32, name="so", tag="so", bufs=2)
-            nc.tensor.transpose(x[:, 0:P], browf[:], ident[:])
-            nc.vector.tensor_copy(out=biasT[:], in_=x[:, 0:P])
-
-        def consts_rest():
-            nc.vector.tensor_copy(out=gf[:], in_=gb[:])
-            nc.vector.tensor_copy(out=bf[:], in_=bb[:])
-
-        def at(n, f):
+        def at(n, f, *args):
             if n in LN_AT:
-                f(LN_AT[n])
+                f(LN_AT[n], *args)
 
-        def out_at(n, f):
+        def out_at(n, f, *args):
             if n in O_AT:
-                f(O_AT[n])
+                f(O_AT[n], *args)
 
         load_w2()
-        load_w2s()
         load_unit(2)
         load_tgt(0)
-        wid(0, range(4))
+        for t in range(4):
+            wid(0, t)
         widv(0)
         for n in range(NU):
             if n + 3 < NU:
@@ -385,42 +341,55 @@ def tile_mldecoder_pb_w4_kernel(
             if n + 4 in LN_AT and LN_AT[n + 4] > 0:
                 load_ff(LN_AT[n + 4])
                 load_tgt(LN_AT[n + 4])
-            at(n - 1, recip)
-            at(n + 2, xpose_ff)
-            wid(n + 1, (2,))
-            at(n - 2, inter_h)
-            at(n + 1, quant_ff)
-            at(n - 1, norm)
-            if n == 2:
-                consts_rest()
             if n == 0:
-                consts_b2()
-            at(n, resid)
+                consts_early()
+            if n == 2:
+                consts_late()
+            wid(n + 1, 2)
+            at(n + 1, quant_ff)
+            wid(n + 1, 0)
+            at(n - 1, recip)
+            wid(n + 1, 1)
+            at(n + 2, xpose_ff, 0)
+            at(n + 2, evac_ff, 0)
+            at(n + 2, xpose_ff, 1)
+            at(n - 2, inter_h)
+            inter("S", n)
+            at(n, resid, 0)
+            at(n, resid, 1)
+            at(n - 1, norm)
+            at(n - 1, xpose_z, 0)
+            at(n + 1, stage1, 0)
+            at(n - 1, xpose_z, 1)
+            out_at(n - 1, evac_out, 0)
+            out_at(n - 1, evac_out, 1)
+            at(n - 1, evac_h, 0)
+            at(n + 1, tgt_mm, 0)
+            at(n + 2, evac_ff, 1)
+            at(n, negmean)
+            at(n, square)
             if n > 0:
                 quant_dup(n - 1)
-            wid(n + 1, (0,))
-            at(n, negmean)
-            at(n - 1, xpose_z)
-            inter_s(n)
-            widv(n + 1)
-            at(n - 1, evac_h)
-            out_at(n - 1, evac_out)
-            at(n + 2, evac_ff)
-            at(n + 1, stage1)
             out_at(n - 1, xpose_out)
-            at(n, square)
-            wid(n + 1, (1,))
-            inter_dup(n)
-            at(n + 1, tgt_mm)
-            at(n + 1, tgtb)
+            at(n - 1, evac_h, 1)
             out_at(n - 1, copy_out)
-            wid(n + 1, (3,))
+            at(n + 1, tgtb, 0)
             at(n - 2, quant_h)
-            out_at(n, stage2)
-        quant_dup(NU - 1, (0, 1))
-        stage2(NT - 1, (0,))
-        quant_dup(NU - 1, (1, 2))
-        stage2(NT - 1, (1,))
-        evac_out(NT - 1)
+            inter("V", n)
+            at(n + 1, tgt_mm, 1)
+            at(n + 1, stage1, 1)
+            at(n + 1, stage1, 2)
+            at(n + 1, tgtb, 1)
+            wid(n + 1, 3)
+            at(n + 1, stage1, 3)
+            out_at(n, stage2, 0)
+            out_at(n, stage2, 1)
+            widv(n + 1)
+        quant_dup(NU - 1, 0, 512)
+        stage2(NT - 1, 0)
+        quant_dup(NU - 1, 512, 1024)
+        stage2(NT - 1, 1)
+        evac_out(NT - 1, 0)
+        evac_out(NT - 1, 1)
         xpose_out(NT - 1)
         copy_out(NT - 1)

@@ -25,9 +25,9 @@ EPS = 1e-5
 S_OF = [2,5,6,7,8,9,11,12]
 LN_AT = {S_OF[T]: T for T in range(NT)}
 O_AT = {max(2 * T + 2, S_OF[T] + 2): T for T in range(NT)}
-EARLY = 3
-V_PLANES = [6,4,6,1,3,1,0,2,0,3,1,0,1,2,0,0]
-S_KLS = [1,2,0,1,2,0,0,0,2,0,0,0,1,1,1,4]
+WIDE_ROWS = [1,1,1,1,0,1,0,0,0,0,0,0,0,0,0,0]
+V_PLANES = [2,2,2,2,2,2,0,3,0,3,2,0,2,2,0,0]
+S_KLS = [1,1,2,2,2,0,0,0,2,1,1,2,2,1,0,4]
 
 
 def tile_mldecoder_pb_w4_kernel(
@@ -52,10 +52,10 @@ def tile_mldecoder_pb_w4_kernel(
 
         def load_unit(n, parts=1):
             src = dup_g[n // 2][n % 2]
-            if n < EARLY:
+            if WIDE_ROWS[n]:
                 w = KL // parts
                 for q in range(parts):
-                    r = sb.tile([P, w * 4 * G], U8, name="raw", tag="raw" + str(parts), bufs=max(parts, EARLY - 1), align_bytes=64)
+                    r = sb.tile([P, w * 4 * G], U8, name="raw", tag="raw" + str(parts), bufs=3 if parts == 1 else parts, align_bytes=64)
                     nc.sync.dma_start(out=r[:].rearrange("p (kl x) -> p kl x", kl=w), in_=src[:, w * q : w * (q + 1), :])
                     for j in range(w):
                         for t in range(4):
@@ -101,6 +101,7 @@ def tile_mldecoder_pb_w4_kernel(
         gf = keep.tile([P, 2, 4], F32, name="gf")
         bf = keep.tile([P, 2, 4], F32, name="bf")
         cols = keep.tile([P, P], F32, name="cols")
+        b2w = keep.tile([P, 8, P], F32, name="b2w")
         browf = keep.tile([P, P], F32, name="browf")
         identb = keep.tile([P, P], BF16, name="identb")
 
@@ -118,6 +119,7 @@ def tile_mldecoder_pb_w4_kernel(
             x = psum.tile([P, 512], F32, name="so", tag="so", bufs=2)
             nc.tensor.transpose(x[:, 0:P], browf[:], ident[:])
             nc.vector.tensor_copy(out=cols[:], in_=x[:, 0:P])
+            nc.vector.tensor_copy(out=b2w[:], in_=cols[:, K : K + 8].unsqueeze(2).to_broadcast([P, 8, P]))
 
         def consts_late():
             nc.vector.tensor_copy(out=gf[:], in_=gb[:])
@@ -136,8 +138,8 @@ def tile_mldecoder_pb_w4_kernel(
         def widen_part(eng, n, t):
             if n >= NU:
                 return
-            if n < EARLY:
-                vk = V_PLANES[n]
+            if WIDE_ROWS[n]:
+                vk = 2 * V_PLANES[n]
                 for kl in (range(0, KL - vk) if eng == "S" else range(KL - vk, KL)):
                     widen(eng, n, t, slice(G * kl, G * (kl + 1)), raw[n, t, kl])
             elif (eng == "V") == (t >= 4 - V_PLANES[n]):
@@ -179,15 +181,15 @@ def tile_mldecoder_pb_w4_kernel(
 
         def evac_ff(T, j):
             if T not in xg:
-                xg[T] = sb.tile([P, 4 * P * 4], BF16, name="xg", tag="xg", bufs=2, align_bytes=64)
+                xg[T] = sb.tile([P, 4 * P * 4], BF16, name="xg", tag="xg", bufs=3, align_bytes=64)
             nc.scalar.copy(
                 out=xg[T][:, 1024 * j : 1024 * (j + 1)].bitcast(F32).rearrange("p (g r u) -> p g r u", g=2, u=2),
                 in_=xt[T, j][:].rearrange("p (g u r) -> p g r u", g=2, u=2),
             )
 
         def quant_ff(T):
-            fc[T] = sb.tile([P, 4 * P], U32, name="fc", tag="fc", bufs=2, align_bytes=64)
-            fs[T] = sb.tile([P, 4 * P], U8, name="fs", tag="fs", bufs=2, align_bytes=64)
+            fc[T] = sb.tile([P, 4 * P], U32, name="fc", tag="fc", bufs=3, align_bytes=64)
+            fs[T] = sb.tile([P, 4 * P], U8, name="fs", tag="fs", bufs=3, align_bytes=64)
             nc.vector.quantize_mx(out=fc[T][:].bitcast(FP8X4), scales=fs[T][:], in_=xg[T][:])
 
         def stage1(T, part):
@@ -209,16 +211,16 @@ def tile_mldecoder_pb_w4_kernel(
             x = psum.tile([P, 512], F32, name="xt", tag="xt", bufs=2)
             nc.tensor.matmul(x[:], lhsT=identb[:], rhs=tg[T][:, 512 * h : 512 * (h + 1)], start=True, stop=False)
             for c in range(4):
-                col = K + 4 * h + c
+                col = 4 * h + c
                 nc.tensor.matmul(
-                    x[:, P * c : P * (c + 1)], lhsT=cols[:, col : col + 1].to_broadcast([P, P]), rhs=ident[:],
+                    x[:, P * c : P * (c + 1)], lhsT=b2w[:, col, :], rhs=ident[:],
                     is_transpose=True, start=False, stop=(c == 3),
                 )
             tp[T, h] = x
 
         def tgtb(T, h):
             if T not in tb:
-                tb[T] = sb.tile([P, D], F32, name="tb", tag="tb", bufs=2, align_bytes=64)
+                tb[T] = sb.tile([P, D], F32, name="tb", tag="tb", bufs=3, align_bytes=64)
             nc.scalar.copy(
                 out=tb[T][:, 512 * h : 512 * (h + 1)].rearrange("p (t q) -> p t q", t=4),
                 in_=tp[T, h][:].rearrange("p (q t) -> p t q", t=4),
@@ -341,50 +343,50 @@ def tile_mldecoder_pb_w4_kernel(
             if n + 4 in LN_AT and LN_AT[n + 4] > 0:
                 load_ff(LN_AT[n + 4])
                 load_tgt(LN_AT[n + 4])
-            if n == 0:
+            if n == 1:
                 consts_early()
             if n == 2:
                 consts_late()
-            wid(n + 1, 2)
             at(n + 1, quant_ff)
+            wid(n + 1, 1)
+            at(n + 2, xpose_ff, 1)
+            at(n, resid, 0)
             wid(n + 1, 0)
             at(n - 1, recip)
-            wid(n + 1, 1)
-            at(n + 2, xpose_ff, 0)
-            at(n + 2, evac_ff, 0)
-            at(n + 2, xpose_ff, 1)
-            at(n - 2, inter_h)
-            inter("S", n)
-            at(n, resid, 0)
             at(n, resid, 1)
-            at(n - 1, norm)
-            at(n - 1, xpose_z, 0)
-            at(n + 1, stage1, 0)
-            at(n - 1, xpose_z, 1)
-            out_at(n - 1, evac_out, 0)
             out_at(n - 1, evac_out, 1)
-            at(n - 1, evac_h, 0)
-            at(n + 1, tgt_mm, 0)
-            at(n + 2, evac_ff, 1)
+            at(n + 2, xpose_ff, 0)
+            at(n - 2, inter_h)
+            at(n - 1, norm)
+            at(n + 1, stage1, 0)
+            at(n + 1, stage1, 1)
             at(n, negmean)
-            at(n, square)
             if n > 0:
                 quant_dup(n - 1)
+            at(n + 2, evac_ff, 1)
+            at(n - 1, xpose_z, 1)
+            at(n + 2, evac_ff, 0)
+            at(n - 1, xpose_z, 0)
+            inter("S", n)
+            at(n + 1, tgt_mm, 0)
+            out_at(n - 1, evac_out, 0)
+            wid(n + 1, 2)
+            at(n - 1, evac_h, 0)
             out_at(n - 1, xpose_out)
-            at(n - 1, evac_h, 1)
-            out_at(n - 1, copy_out)
-            at(n + 1, tgtb, 0)
-            at(n - 2, quant_h)
-            inter("V", n)
             at(n + 1, tgt_mm, 1)
-            at(n + 1, stage1, 1)
+            at(n, square)
+            at(n - 2, quant_h)
+            at(n + 1, tgtb, 0)
             at(n + 1, stage1, 2)
-            at(n + 1, tgtb, 1)
-            wid(n + 1, 3)
+            at(n - 1, evac_h, 1)
+            inter("V", n)
+            out_at(n - 1, copy_out)
             at(n + 1, stage1, 3)
-            out_at(n, stage2, 0)
+            at(n + 1, tgtb, 1)
             out_at(n, stage2, 1)
             widv(n + 1)
+            wid(n + 1, 3)
+            out_at(n, stage2, 0)
         quant_dup(NU - 1, 0, 512)
         stage2(NT - 1, 0)
         quant_dup(NU - 1, 512, 1024)

from contextlib import ExitStack

import concourse.mybir as mybir
from concourse.masks import make_identity

B, K, G, D, FF = 16, 64, 128, 1024, 2048
FLOPS = 2 * B * K * FF * D + 2 * B * K * D * G

F32 = mybir.dt.float32
BF16 = mybir.dt.bfloat16
U32 = mybir.dt.uint32
I32 = mybir.dt.int32
U8 = mybir.dt.uint8
FP8 = mybir.dt.float8_e4m3fn
FP8X4 = mybir.dt.float8_e4m3fn_x4
FP4X4 = mybir.dt.float4_e2m1fn_x4
ACT = mybir.ActivationFunctionType
ALU = mybir.AluOpType

P = 128
NT = 8
KL = 8
NU = 2 * NT
EPS = 1e-5
S_OF = [2,5,6,7,8,9,11,12]
LN_AT = {S_OF[T]: T for T in range(NT)}
O_AT = {max(2 * T + 2, S_OF[T] + 2): T for T in range(NT)}
WIDE_ROWS = [1,1,1,1,0,1,0,0,0,0,0,0,0,0,0,0]
V_PLANES = [2,2,2,2,2,2,0,3,0,3,2,0,2,2,0,0]
S_KLS = [1,1,2,2,2,0,0,0,2,1,1,2,2,1,0,4]


def tile_mldecoder_pb_w4_kernel(
    tc, ff_hid, tgt, w2_words, w2_scales, b2, g3, be3, dup_pool_bytes, dup_pool_scale, dup_bias, out
):
    nc = tc.nc
    ff_g = ff_hid.rearrange("b k f -> (b k) f").rearrange("(m kt) f -> kt m f", kt=NT)
    tgt_g = tgt.rearrange("b k f -> (b k) f").rearrange("(m kt) f -> kt m f", kt=NT)
    dup_g = dup_pool_bytes.rearrange("(kl kt) (g p t) n -> kt g p kl (t n)", kt=NT, g=2, t=4)
    out_g = out.rearrange("b (kl kt g) -> kt (b kl) g", kt=NT, kl=KL)

    with ExitStack() as ctx:
        keep = ctx.enter_context(tc.tile_pool(name="keep", bufs=1))
        sb = ctx.enter_context(tc.tile_pool(name="sb", bufs=2))
        psum = ctx.enter_context(tc.psum_pool(name="psum", bufs=2))
        ctx.enter_context(tc.manual_schedule())

        raw, xf, tg, wd, gd, dc, ds = {}, {}, {}, {}, {}, {}, {}
        xt, xg, fc, fs, acc, tb, tp = {}, {}, {}, {}, {}, {}, {}
        us, sm, nm, sd, rs, zs, ht, hp, hg, hc, hs = {}, {}, {}, {}, {}, {}, {}, {}, {}, {}, {}
        so, res, oT = {}, {}, {}

        def load_unit(n, parts=1):
            src = dup_g[n // 2][n % 2]
            if WIDE_ROWS[n]:
                w = KL // parts
                for q in range(parts):
                    r = sb.tile([P, w * 4 * G], U8, name="raw", tag="raw" + str(parts), bufs=3 if parts == 1 else parts, align_bytes=64)
                    nc.sync.dma_start(out=r[:].rearrange("p (kl x) -> p kl x", kl=w), in_=src[:, w * q : w * (q + 1), :])
                    for j in range(w):
                        for t in range(4):
                            raw[n, t, w * q + j] = r[:, G * (4 * j + t) : G * (4 * j + t + 1)]
            else:
                for t in range(4):
                    r = sb.tile([P, KL * G], U8, name="rawt", tag="rawt", bufs=16, align_bytes=64)
                    nc.sync.dma_start(
                        out=r[:].rearrange("p (kl n) -> p kl n", kl=KL), in_=src[:, :, G * t : G * (t + 1)]
                    )
                    raw[n, t] = r[:]

        def load_ff(T):
            xf[T] = sb.tile([P, FF], BF16, name="xf", tag="xf", bufs=4, align_bytes=64)
            nc.sync.dma_start(out=xf[T][:], in_=ff_g[T])

        def load_tgt(T):
            tg[T] = sb.tile([P, D], BF16, name="tg", tag="tg", bufs=4, align_bytes=64)
            nc.sync.dma_start(out=tg[T][:], in_=tgt_g[T])

        ident = keep.tile([P, P], F32, name="ident")
        make_identity(nc, ident[:])
        ones = keep.tile([P, 1], BF16, name="ones")
        nc.vector.memset(ones[:], 1.0)
        warm = keep.tile([P, 1], F32, name="warm")
        nc.scalar.activation(out=warm[:], in_=ones[:], func=ACT.Sqrt)
        brow = keep.tile([P, P], BF16, name="brow", align_bytes=64)
        nc.vector.memset(brow[:], 0.0)
        nc.gpsimd.dma_start(out=brow[K : K + 8, :], in_=b2.rearrange("(c n) -> c n", n=P))
        nc.gpsimd.dma_start(out=brow[0:K, :], in_=dup_bias.rearrange("(k g) -> k g", g=G))
        dsc = keep.tile([P, 2, 4], F32, name="dsc")
        nc.sync.dma_start(out=dsc[:], in_=dup_pool_scale.rearrange("o (g p t) u -> p (o g) (t u)", g=2, t=4))
        load_unit(0, 2)
        load_ff(0)
        load_unit(1)
        gb = keep.tile([P, 2, 4], BF16, name="gb")
        bb = keep.tile([P, 2, 4], BF16, name="bb")
        nc.scalar.dma_start(out=gb[:], in_=g3.rearrange("(g p t) -> p g t", g=2, t=4))
        nc.scalar.dma_start(out=bb[:], in_=be3.rearrange("(g p t) -> p g t", g=2, t=4))
        w2w = keep.tile([P, 4, 2 * D], U8, name="w2w", align_bytes=64)
        w2s = keep.tile([P, 4, D], U8, name="w2s", align_bytes=64)
        nc.vector.memset(w2s[:].rearrange("p g n -> p (g n)").bitcast(I32), 0)
        gf = keep.tile([P, 2, 4], F32, name="gf")
        bf = keep.tile([P, 2, 4], F32, name="bf")
        cols = keep.tile([P, P], F32, name="cols")
        b2w = keep.tile([P, 8, P], F32, name="b2w")
        browf = keep.tile([P, P], F32, name="browf")
        identb = keep.tile([P, P], BF16, name="identb")

        def load_w2():
            nc.sync.dma_start(out=w2w[:], in_=w2_words.rearrange("g p n -> p g n"))
            for q in range(4):
                nc.sync.dma_start(
                    out=w2s[32 * q : 32 * q + 4, :, :].bitcast(I32),
                    in_=w2_scales[:, 4 * q : 4 * q + 4, :].rearrange("g q n -> q g n").bitcast(I32),
                )

        def consts_early():
            nc.vector.tensor_copy(out=browf[:], in_=brow[:])
            nc.vector.tensor_copy(out=identb[:], in_=ident[:])
            x = psum.tile([P, 512], F32, name="so", tag="so", bufs=2)
            nc.tensor.transpose(x[:, 0:P], browf[:], ident[:])
            nc.vector.tensor_copy(out=cols[:], in_=x[:, 0:P])
            nc.vector.tensor_copy(out=b2w[:], in_=cols[:, K : K + 8].unsqueeze(2).to_broadcast([P, 8, P]))

        def consts_late():
            nc.vector.tensor_copy(out=gf[:], in_=gb[:])
            nc.vector.tensor_copy(out=bf[:], in_=bb[:])

        def widen(eng, n, t, dst_cols, src):
            if n not in wd:
                wd[n] = sb.tile([P, 4, KL * G], BF16, name="wd", tag="wd", bufs=3, align_bytes=64)
            dst = wd[n][:, t, dst_cols]
            scale = dsc[:, n % 2, t : t + 1]
            if eng == "S":
                nc.scalar.activation(out=dst, in_=src.bitcast(FP8), func=ACT.Copy, scale=scale)
            else:
                nc.vector.tensor_scalar(out=dst, in0=src.bitcast(FP8), scalar1=scale, scalar2=None, op0=ALU.mult)

        def widen_part(eng, n, t):
            if n >= NU:
                return
            if WIDE_ROWS[n]:
                vk = 2 * V_PLANES[n]
                for kl in (range(0, KL - vk) if eng == "S" else range(KL - vk, KL)):
                    widen(eng, n, t, slice(G * kl, G * (kl + 1)), raw[n, t, kl])
            elif (eng == "V") == (t >= 4 - V_PLANES[n]):
                widen(eng, n, t, slice(0, KL * G), raw[n, t])

        def wid(n, t):
            widen_part("S", n, t)

        def widv(n):
            for t in range(4):
                widen_part("V", n, t)

        def inter(eng, n):
            if n not in gd:
                gd[n] = sb.tile([P, KL * G * 4], BF16, name="gd", tag="gd", bufs=3, align_bytes=64)
            k0, k1 = (0, KL - S_KLS[n]) if eng == "V" else (KL - S_KLS[n], KL)
            if k0 < k1:
                dst = gd[n][:, 4 * G * k0 : 4 * G * k1].rearrange("p (c i t) -> p c t i", i=4, t=4)
                src = wd[n][:, :, G * k0 : G * k1].rearrange("p t (c i) -> p c t i", i=4)
                if eng == "S":
                    nc.scalar.copy(out=dst, in_=src)
                else:
                    nc.vector.tensor_copy(out=dst, in_=src)

        def quant_dup(n, lo=0, hi=KL * G):
            if n not in dc:
                dc[n] = sb.tile([P, KL * G], U32, name="dc", tag="dc", bufs=8, align_bytes=64)
                ds[n] = sb.tile([P, KL * G], U8, name="ds", tag="ds", bufs=8, align_bytes=64)
            nc.vector.quantize_mx(
                out=dc[n][:, lo:hi].bitcast(FP8X4), scales=ds[n][:, lo:hi], in_=gd[n][:, 4 * lo : 4 * hi]
            )

        def xpose_ff(T, j):
            words = xf[T][:].bitcast(F32)
            xt[T, j] = psum.tile([P, 512], F32, name="xt", tag="xt", bufs=2)
            for i in range(4):
                lo = 256 * (2 * j + i // 2) + i % 2
                nc.tensor.transpose(xt[T, j][:, P * i : P * (i + 1)], words[:, lo : lo + 255 : 2], ident[:])

        def evac_ff(T, j):
            if T not in xg:
                xg[T] = sb.tile([P, 4 * P * 4], BF16, name="xg", tag="xg", bufs=3, align_bytes=64)
            nc.scalar.copy(
                out=xg[T][:, 1024 * j : 1024 * (j + 1)].bitcast(F32).rearrange("p (g r u) -> p g r u", g=2, u=2),
                in_=xt[T, j][:].rearrange("p (g u r) -> p g r u", g=2, u=2),
            )

        def quant_ff(T):
            fc[T] = sb.tile([P, 4 * P], U32, name="fc", tag="fc", bufs=3, align_bytes=64)
            fs[T] = sb.tile([P, 4 * P], U8, name="fs", tag="fs", bufs=3, align_bytes=64)
            nc.vector.quantize_mx(out=fc[T][:].bitcast(FP8X4), scales=fs[T][:], in_=xg[T][:])

        def stage1(T, part):
            h = part // 2
            if part % 2 == 0:
                acc[T, h] = psum.tile([P, 512], F32, name="acc", tag="acc", bufs=2)
            for g in (0, 1) if part % 2 == 0 else (2, 3):
                nc.tensor.matmul_mx(
                    out=acc[T, h][:],
                    lhsT=fc[T][:, P * g : P * (g + 1)].bitcast(FP8X4),
                    lhsT_scale=fs[T][:, P * g : P * (g + 1)],
                    rhs=w2w[:, g, 1024 * h : 1024 * (h + 1)].bitcast(FP4X4),
                    rhs_scale=w2s[:, g, 512 * h : 512 * (h + 1)],
                    start=(g == 0),
                    stop=(g == 3),
                )

        def tgt_mm(T, h):
            x = psum.tile([P, 512], F32, name="xt", tag="xt", bufs=2)
            nc.tensor.matmul(x[:], lhsT=identb[:], rhs=tg[T][:, 512 * h : 512 * (h + 1)], start=True, stop=False)
            for c in range(4):
                col = 4 * h + c
                nc.tensor.matmul(
                    x[:, P * c : P * (c + 1)], lhsT=b2w[:, col, :], rhs=ident[:],
                    is_transpose=True, start=False, stop=(c == 3),
                )
            tp[T, h] = x

        def tgtb(T, h):
            if T not in tb:
                tb[T] = sb.tile([P, D], F32, name="tb", tag="tb", bufs=3, align_bytes=64)
            nc.scalar.copy(
                out=tb[T][:, 512 * h : 512 * (h + 1)].rearrange("p (t q) -> p t q", t=4),
                in_=tp[T, h][:].rearrange("p (q t) -> p t q", t=4),
            )

        def resid(T, h):
            if T not in us:
                us[T] = sb.tile([P, D], F32, name="us", tag="us", bufs=2, align_bytes=64)
            half = slice(512 * h, 512 * (h + 1))
            sm[T, h] = sb.tile([P, 1], F32, name="sum", tag="sum", bufs=4)
            nc.vector.scalar_tensor_tensor(
                out=us[T][:, half].rearrange("p (t q) -> p t q", t=4),
                in0=acc[T, h][:].rearrange("p (q t) -> p t q", t=4), scalar=0.0,
                in1=tb[T][:, half].rearrange("p (t q) -> p t q", t=4),
                op0=ALU.add, op1=ALU.add, accum_out=sm[T, h][:],
            )

        def negmean(T):
            nm[T] = sb.tile([P, 1], F32, name="nm", tag="nm", bufs=3)
            nc.vector.tensor_scalar(
                out=nm[T][:], in0=sm[T, 0][:], scalar1=sm[T, 1][:], scalar2=-1.0 / D, op0=ALU.add, op1=ALU.mult
            )

        def square(T):
            junk = sb.tile([P, D], F32, name="junk", tag="junk", bufs=1)
            ss = sb.tile([P, 1], F32, name="ss", tag="ss", bufs=2)
            nc.scalar.activation(out=junk[:], in_=us[T][:], func=ACT.Square, bias=nm[T][:], accum_out=ss[:])
            sd[T] = sb.tile([P, 1], F32, name="sd", tag="sd", bufs=2)
            nc.scalar.activation(out=sd[T][:], in_=ss[:], func=ACT.Sqrt, scale=1.0 / D, bias=EPS)

        def recip(T):
            rs[T] = sb.tile([P, 1], F32, name="rs", tag="rs", bufs=2)
            nc.vector.reciprocal(out=rs[T][:], in_=sd[T][:])

        def norm(T):
            zs[T] = sb.tile([P, D], F32, name="zs", tag="zs", bufs=2, align_bytes=64)
            nc.vector.tensor_scalar(
                out=zs[T][:], in0=us[T][:], scalar1=nm[T][:], scalar2=rs[T][:], op0=ALU.add, op1=ALU.mult
            )

        def xpose_z(T, g):
            ht[T, g] = psum.tile([P, 512], F32, name="ht", tag="ht", bufs=2)
            for t in range(4):
                lo = 512 * g + P * t
                nc.tensor.transpose(ht[T, g][:, P * t : P * (t + 1)], zs[T][:, lo : lo + P], ident[:])

        def evac_h(T, g):
            if T not in hp:
                hp[T] = sb.tile([P, 2, 4, P], BF16, name="hp", tag="hp", bufs=2, align_bytes=64)
            for t in range(4):
                nc.scalar.activation(
                    out=hp[T][:, g, t, :], in_=ht[T, g][:, P * t : P * (t + 1)], func=ACT.Identity,
                    scale=gf[:, g, t : t + 1], bias=bf[:, g, t : t + 1],
                )

        def inter_h(T):
            hg[T] = sb.tile([P, 2 * P * 4], BF16, name="hg", tag="hg", bufs=2, align_bytes=64)
            for g in range(2):
                nc.vector.tensor_copy(
                    out=hg[T][:, 512 * g : 512 * (g + 1)].rearrange("p (kl b t) -> p kl b t", kl=KL, t=4),
                    in_=hp[T][:, g, :, :].rearrange("p t (b kl) -> p kl b t", kl=KL),
                )

        def quant_h(T):
            hc[T] = sb.tile([P, 2 * P], U32, name="hc", tag="hc", bufs=4, align_bytes=64)
            hs[T] = sb.tile([P, 2 * P], U8, name="hs", tag="hs", bufs=4, align_bytes=64)
            nc.vector.quantize_mx(out=hc[T][:].bitcast(FP8X4), scales=hs[T][:], in_=hg[T][:])

        def stage2(T, h):
            so[T, h] = psum.tile([P, 512], F32, name="so", tag="so", bufs=2)
            for j in range(4):
                kl = 4 * h + j
                for g in range(2):
                    nc.tensor.matmul_mx(
                        out=so[T, h][:, P * j : P * (j + 1)],
                        lhsT=dc[2 * T + g][:, P * kl : P * (kl + 1)].bitcast(FP8X4),
                        lhsT_scale=ds[2 * T + g][:, P * kl : P * (kl + 1)],
                        rhs=hc[T][:, P * g : P * (g + 1)].bitcast(FP8X4),
                        rhs_scale=hs[T][:, P * g : P * (g + 1)],
                        start=(g == 0),
                        stop=(g == 1),
                    )

        def evac_out(T, h):
            if T not in res:
                res[T] = sb.tile([P, P], F32, name="res", tag="res", bufs=2, align_bytes=64)
            v = so[T, h][:, 64 * h : 64 * h + 448].rearrange("p (a c) -> p a c", c=16)[:, 0:28:9, :]
            bias = cols[:, 0:K].rearrange("p (kl kt) -> p kl kt", kt=NT)[:, 4 * h : 4 * h + 4, T : T + 1]
            nc.vector.tensor_tensor(
                out=res[T][:].rearrange("p (b kl) -> p kl b", kl=KL)[:, 4 * h : 4 * h + 4, :],
                in0=v, in1=bias.to_broadcast([P, 4, B]), op=ALU.add,
            )

        def xpose_out(T):
            oT[T] = psum.tile([P, 512], F32, name="so", tag="so", bufs=2)
            nc.tensor.transpose(oT[T][:, 0:P], res[T][:], ident[:])

        def copy_out(T):
            y = sb.tile([P, G], F32, name="ot", tag="ot", bufs=2, align_bytes=64)
            nc.scalar.copy(out=y[:], in_=oT[T][:, 0:P])
            nc.scalar.dma_start(out=out_g[T], in_=y[:])

        def at(n, f, *args):
            if n in LN_AT:
                f(LN_AT[n], *args)

        def out_at(n, f, *args):
            if n in O_AT:
                f(O_AT[n], *args)

        load_w2()
        load_unit(2)
        load_tgt(0)
        for t in range(4):
            wid(0, t)
        widv(0)
        for n in range(NU):
            if n + 3 < NU:
                load_unit(n + 3)
            if n + 4 in LN_AT and LN_AT[n + 4] > 0:
                load_ff(LN_AT[n + 4])
                load_tgt(LN_AT[n + 4])
            if n == 1:
                consts_early()
            if n == 2:
                consts_late()
            at(n + 1, quant_ff)
            wid(n + 1, 1)
            at(n + 2, xpose_ff, 1)
            at(n, resid, 0)
            wid(n + 1, 0)
            at(n - 1, recip)
            at(n, resid, 1)
            out_at(n - 1, evac_out, 1)
            at(n + 2, xpose_ff, 0)
            at(n - 2, inter_h)
            at(n - 1, norm)
            at(n + 1, stage1, 0)
            at(n + 1, stage1, 1)
            at(n, negmean)
            if n > 0:
                quant_dup(n - 1)
            at(n + 2, evac_ff, 1)
            at(n - 1, xpose_z, 1)
            at(n + 2, evac_ff, 0)
            at(n - 1, xpose_z, 0)
            inter("S", n)
            at(n + 1, tgt_mm, 0)
            out_at(n - 1, evac_out, 0)
            wid(n + 1, 2)
            at(n - 1, evac_h, 0)
            out_at(n - 1, xpose_out)
            at(n + 1, tgt_mm, 1)
            at(n, square)
            at(n - 2, quant_h)
            at(n + 1, tgtb, 0)
            at(n + 1, stage1, 2)
            at(n - 1, evac_h, 1)
            inter("V", n)
            out_at(n - 1, copy_out)
            at(n + 1, stage1, 3)
            at(n + 1, tgtb, 1)
            out_at(n, stage2, 1)
            widv(n + 1)
            wid(n + 1, 3)
            out_at(n, stage2, 0)
        quant_dup(NU - 1, 0, 512)
        stage2(NT - 1, 0)
        quant_dup(NU - 1, 512, 1024)
        stage2(NT - 1, 1)
        evac_out(NT - 1, 0)
        evac_out(NT - 1, 1)
        xpose_out(NT - 1)
        copy_out(NT - 1)
